import numpy as np
import ml_dtypes


def mxq(x, axis, fmt="e4m3"):
    dtype, down = {"e4m3": (ml_dtypes.float8_e4m3fn, 7), "e5m2": (ml_dtypes.float8_e5m2, 14)}[fmt]
    v = np.moveaxis(np.asarray(x, np.float32).astype(ml_dtypes.bfloat16).astype(np.float64), axis, -1)
    blocks = v.reshape(v.shape[:-1] + (-1, 32))
    amax = np.abs(blocks).max(-1, keepdims=True)
    byte = np.maximum(np.where(amax > 0, np.frexp(amax)[1] - 1 + 127, 0) - down, 1)
    scale = np.exp2(byte - 127.0)
    codes = (blocks / scale).astype(np.float32).astype(dtype).astype(np.float64)
    return np.moveaxis((codes * scale).reshape(v.shape), -1, axis)


WIDE = False


def mx_kscale(k):
    if not WIDE:
        return np.ones(k)
    levels = np.array([10, -10, 5, -5, 0])
    a = np.random.permutation(np.resize(levels, k // 512 * 4)).reshape(k // 512, 4)
    idx = np.arange(k)
    return np.exp2(a[idx // 512, idx % 128 // 32])


BF16 = ml_dtypes.bfloat16


def bf(x):
    return np.asarray(x, np.float32).astype(BF16)


def f64(x):
    return np.asarray(x).astype(np.float64)


B, NH, D, HH, WW = 1, 4, 128, 32, 32
C = NH * D
S = HH * WW


def _masked_softmax(x, mask):
    m = 1.0 - mask / -10000.0
    x = x * m + (1.0 - m) * np.min(x)
    x = x - np.max(x, axis=-1, keepdims=True)
    e = np.exp(x) * m
    return e / np.sum(e, axis=-1, keepdims=True)


def setup_inputs():
    s = mx_kscale(S).reshape(HH, WW)
    q = np.random.standard_normal((B, C, HH, WW))
    k = np.random.standard_normal((B, C, HH, WW))
    v = np.random.standard_normal((B, C, HH, WW)) * 3.0
    q[:, ::D] = np.log(2.0) * np.sqrt(D)
    k[:, ::D] -= np.log2(s)
    v = v * s * 2.0 ** np.round(np.log2(np.mean(1.0 / s)))
    return {"q": bf(q), "k": bf(k), "v": bf(v),
            "attn_mask": bf(np.random.random_sample((B, S, S)) * -10000.0)}


def reference(q, k, v, attn_mask):
    def to_seq(x):
        return x.reshape(B * NH, D, S).swapaxes(-1, -2)

    qs, ks, vs = to_seq(f64(q)), to_seq(f64(k)), to_seq(f64(v))
    scale = D ** (-0.5)
    mask = np.repeat(f64(attn_mask), NH, axis=0)
    scores = (qs @ ks.swapaxes(-1, -2)) * scale
    attn = _masked_softmax(scores, mask)
    out = mxq(attn, 2, "e4m3") @ mxq(vs, 1, "e4m3")
    return out.swapaxes(-1, -2).reshape(B, C, HH, WW)

@@ -1,0 +1,216 @@
+from contextlib import ExitStack
+
+import concourse.mybir as mybir
+from concourse.masks import make_identity
+
+F32 = mybir.dt.float32
+BF16 = mybir.dt.bfloat16
+U32 = mybir.dt.uint32
+U8 = mybir.dt.uint8
+FP8X4 = mybir.dt.float8_e4m3fn_x4
+ALU = mybir.AluOpType
+ACT = mybir.ActivationFunctionType
+AX = mybir.AxisListType
+
+P = 128
+NH = 4
+D = 128
+S = 1024
+NT = S // P
+HALF = 512
+SCALE = D ** -0.5
+FLOPS = 2 * 2 * NH * S * S * D
+MANUAL = True
+
+
+def tile_mhattention_own_kernel(tc, q, k, v, attn_mask, out):
+    nc = tc.nc
+    qv = q.rearrange("b c h w -> (b c) (h w)").rearrange("(n d) s -> d n s", d=D)
+    kv = k.rearrange("b c h w -> (b c) (h w)").rearrange("(n d) s -> d n s", d=D)
+    vv = v.rearrange("b c h w -> (b c) (h w)").rearrange("(n d) s -> d n s", d=D)
+    ov = out.rearrange("b c h w -> (b c) (h w)").rearrange("(n d) s -> d n s", d=D)
+    mv = attn_mask.rearrange("b i j -> (b i) j").rearrange("(t p) j -> p t j", p=P)
+
+    with ExitStack() as ctx:
+        if MANUAL:
+            ctx.enter_context(tc.manual_schedule())
+        keep = ctx.enter_context(tc.tile_pool(name="keep", bufs=1))
+        ps_g = ctx.enter_context(tc.psum_pool(name="ps_g", bufs=1))
+
+        sn = keep.tile([P, NT, NH, S], F32)
+        m = keep.tile([P, NT, S], F32)
+        vcodes = keep.tile([P, NH * 2 * D], U32, align_bytes=64)
+        vscl = keep.tile([P, NH * 2 * D], U8, align_bytes=64)
+        ident_b = keep.tile([P, P], BF16)
+        ident_f = keep.tile([P, P], F32)
+        gn = keep.tile([P, 1], F32)
+        zero = keep.tile([P, 1], F32)
+        warm = keep.tile([P, 1], F32)
+
+        make_identity(nc, ident_b[:])
+        make_identity(nc, ident_f[:])
+        nc.vector.memset(zero[:], 0.0)
+        nc.scalar.activation(out=warm[:], in_=zero[:], func=ACT.Exp)
+
+        with ExitStack() as c1:
+            p1 = c1.enter_context(tc.tile_pool(name="p1", bufs=1))
+            ps_a = c1.enter_context(tc.psum_pool(name="ps_a", bufs=4))
+            ps_v = c1.enter_context(tc.psum_pool(name="ps_v", bufs=2))
+            q_sb = p1.tile([P, NH, S], BF16)
+            k_sb = p1.tile([P, NH, S], BF16)
+            v_sb = p1.tile([P, NH, S], BF16)
+            mk = p1.tile([P, NT, S], BF16)
+            gv = p1.tile([P, NH, 2, D, 4], BF16, align_bytes=64)
+            rm0 = p1.tile([P, S], F32)
+            rm1 = p1.tile([P, S], F32)
+            gp = p1.tile([P, 1], F32)
+            gb = p1.tile([P, P], F32)
+            rms = [rm0, rm1]
+            nc.vector.memset(rm0[:], -3.0e38)
+            nc.vector.memset(rm1[:], -3.0e38)
+
+            for n in range(NH):
+                nc.sync.dma_start(out=q_sb[:, n, :], in_=qv[:, n, :])
+                nc.sync.dma_start(out=k_sb[:, n, :], in_=kv[:, n, :])
+            nc.sync.dma_start(out=v_sb[:], in_=vv)
+            for t in range(0, NT, 2):
+                nc.sync.dma_start(out=mk[:, t : t + 2, :], in_=mv[:, t : t + 2, :])
+
+            for n in range(NH):
+                for it in range(NT):
+                    for jh in range(2):
+                        ps = ps_a.tile([P, HALF], F32)
+                        nc.tensor.matmul(
+                            out=ps[:],
+                            lhsT=q_sb[:, n, it * P : (it + 1) * P],
+                            rhs=k_sb[:, n, jh * HALF : (jh + 1) * HALF],
+                            start=True,
+                            stop=True,
+                        )
+                        nc.scalar.activation(
+                            out=sn[:, it, n, jh * HALF : (jh + 1) * HALF],
+                            in_=ps[:],
+                            func=ACT.Copy,
+                            scale=-SCALE,
+                        )
+                    rm = rms[it % 2]
+                    nc.vector.tensor_tensor(out=rm[:], in0=sn[:, it, n, :], in1=rm[:], op=ALU.max)
+                    if n == 1:
+                        nc.vector.tensor_scalar(
+                            out=m[:, it, :],
+                            in0=mk[:, it, :],
+                            scalar1=1.0e-4,
+                            scalar2=1.0,
+                            op0=ALU.mult,
+                            op1=ALU.add,
+                        )
+                if n == 0:
+                    for h in range(NH):
+                        pv = ps_v.tile([P, S], BF16)
+                        for c in range(NT):
+                            nc.tensor.transpose(
+                                out=pv[:, c * P : (c + 1) * P],
+                                in_=v_sb[:, h, c * P : (c + 1) * P],
+                                identity=ident_b[:],
+                            )
+                        nc.scalar.copy(
+                            out=gv[:, h],
+                            in_=pv[:].rearrange("p (g t d) -> p g d t", g=2, t=4),
+                        )
+                if n == 2:
+                    nc.vector.quantize_mx(
+                        out=vcodes[:].bitcast(FP8X4),
+                        scales=vscl[:],
+                        in_=gv[:].rearrange("p h g d t -> p (h g d t)"),
+                    )
+
+            nc.vector.tensor_tensor(out=rm0[:], in0=rm0[:], in1=rm1[:], op=ALU.max)
+            nc.vector.tensor_reduce(out=gp[:], in_=rm0[:], axis=AX.X, op=ALU.max)
+            nc.vector.tensor_copy(out=gb[:], in_=gp[:, 0:1].to_broadcast([P, P]))
+            pg = ps_g.tile([P, P], F32)
+            nc.tensor.transpose(out=pg[:], in_=gb[:], identity=ident_f[:])
+            nc.vector.tensor_reduce(out=gn[:], in_=pg[:], axis=AX.X, op=ALU.max)
+
+        work = ctx.enter_context(tc.tile_pool(name="work", bufs=3))
+        stat = ctx.enter_context(tc.tile_pool(name="stat", bufs=4))
+        ps_t = ctx.enter_context(tc.psum_pool(name="ps_t", bufs=3))
+        ps_o = ctx.enter_context(tc.psum_pool(name="ps_o", bufs=2))
+        NB = NT * NH
+        st = {}
+
+        def row(rb):
+            return sn[:, rb // NH, rb % NH, :]
+
+        def stage_a(rb):
+            nc.vector.scalar_tensor_tensor(
+                out=row(rb), in0=row(rb), scalar=gn[:, 0:1], in1=m[:, rb // NH, :],
+                op0=ALU.subtract, op1=ALU.mult,
+            )
+            nb = stat.tile([P, 1], F32)
+            nc.vector.tensor_reduce(out=nb[:], in_=row(rb), axis=AX.X, op=ALU.min)
+            nc.scalar.activation(out=row(rb), in_=row(rb), func=ACT.Exp, bias=nb[:, 0:1], scale=-1.0)
+
+        def stage_c(rb):
+            z = stat.tile([P, 1], F32)
+            nc.vector.scalar_tensor_tensor(
+                out=row(rb), in0=row(rb), scalar=1.0, in1=m[:, rb // NH, :],
+                op0=ALU.mult, op1=ALU.mult, accum_out=z[:],
+            )
+            r = stat.tile([P, 1], F32)
+            nc.vector.reciprocal(out=r[:], in_=z[:])
+            at = work.tile([P, S], BF16)
+            nc.scalar.activation(out=at[:], in_=row(rb), func=ACT.Copy, scale=r[:, 0:1])
+            pt = ps_t.tile([P, S], BF16)
+            for c in range(NT):
+                nc.tensor.transpose(
+                    out=pt[:, c * P : (c + 1) * P], in_=at[:, c * P : (c + 1) * P], identity=ident_b[:]
+                )
+            st[("pt", rb)] = pt
+
+        def stage_f(rb):
+            pt = st[("pt", rb)]
+            gr = work.tile([P, S], BF16, align_bytes=64)
+            nc.scalar.copy(
+                out=gr[:].rearrange("p (g i t) -> p g i t", g=2, t=4),
+                in_=pt[:].rearrange("p (g t i) -> p g i t", g=2, t=4),
+            )
+            st[("gr", rb)] = gr
+
+        def stage_g(rb):
+            it, n = rb // NH, rb % NH
+            gr = st[("gr", rb)]
+            cd = work.tile([P, 2 * P], U32, align_bytes=64)
+            sc = work.tile([P, 2 * P], U8, align_bytes=64)
+            nc.vector.quantize_mx(out=cd[:].bitcast(FP8X4), scales=sc[:], in_=gr[:])
+            if n == 0:
+                po_new = ps_o.tile([P, NH * P], F32)
+                st["po"] = po_new
+            po = st["po"]
+            for g in range(2):
+                w = (n * 2 + g) * D
+                nc.tensor.matmul_mx(
+                    out=po[:, n * P : (n + 1) * P],
+                    lhsT=vcodes[:, w : w + D].bitcast(FP8X4),
+                    lhsT_scale=vscl[:, w : w + D],
+                    rhs=cd[:, g * P : (g + 1) * P].bitcast(FP8X4),
+                    rhs_scale=sc[:, g * P : (g + 1) * P],
+                    start=(g == 0),
+                    stop=(g == 1),
+                )
+            if n == NH - 1:
+                ob = work.tile([P, NH * P], F32)
+                nc.scalar.copy(out=ob[:], in_=po[:])
+                nc.sync.dma_start(
+                    out=ov[:, :, it * P : (it + 1) * P],
+                    in_=ob[:].rearrange("p (n i) -> p n i", n=NH),
+                )
+
+        for i in range(NB + 3):
+            if i < NB:
+                stage_a(i)
+            if 0 <= i - 1 < NB:
+                stage_c(i - 1)
+            if 0 <= i - 2 < NB:
+                stage_f(i - 2)
+            if 0 <= i - 3 < NB:
+                stage_g(i - 3)

@@ -13,204 +13,238 @@ ACT = mybir.ActivationFunctionType
 AX = mybir.AxisListType
 
 P = 128
-NH = 4
-D = 128
-S = 1024
-NT = S // P
-HALF = 512
-SCALE = D ** -0.5
-FLOPS = 2 * 2 * NH * S * S * D
-MANUAL = True
+HEADS = 4
+SEQ = 1024
+Q_TILES = SEQ // P
+CHUNKS = SEQ // P
+BANK = 512
+PACK = 4
+PASSES = SEQ // (P * PACK)
+WORDS = PASSES * P
+BLOCKS = Q_TILES * HEADS
+SCALE = P ** -0.5
+FLOPS = 2 * 2 * HEADS * SEQ * SEQ * P
 
 
 def tile_mhattention_own_kernel(tc, q, k, v, attn_mask, out):
     nc = tc.nc
-    qv = q.rearrange("b c h w -> (b c) (h w)").rearrange("(n d) s -> d n s", d=D)
-    kv = k.rearrange("b c h w -> (b c) (h w)").rearrange("(n d) s -> d n s", d=D)
-    vv = v.rearrange("b c h w -> (b c) (h w)").rearrange("(n d) s -> d n s", d=D)
-    ov = out.rearrange("b c h w -> (b c) (h w)").rearrange("(n d) s -> d n s", d=D)
-    mv = attn_mask.rearrange("b i j -> (b i) j").rearrange("(t p) j -> p t j", p=P)
+    q_dram = q.rearrange("b c h w -> (b c) (h w)").rearrange("(n d) s -> d n s", d=P)
+    k_dram = k.rearrange("b c h w -> (b c) (h w)").rearrange("(n d) s -> d n s", d=P)
+    v_dram = v.rearrange("b c h w -> (b c) (h w)").rearrange("(n d) s -> d n s", d=P)
+    out_dram = out.rearrange("b c h w -> (b c) (h w)").rearrange("(n d) s -> d n s", d=P)
+    mask_dram = attn_mask.rearrange("b i j -> (b i) j").rearrange("(t p) j -> p t j", p=P)
 
     with ExitStack() as ctx:
-        if MANUAL:
-            ctx.enter_context(tc.manual_schedule())
+        ctx.enter_context(tc.manual_schedule())
         keep = ctx.enter_context(tc.tile_pool(name="keep", bufs=1))
-        ps_g = ctx.enter_context(tc.psum_pool(name="ps_g", bufs=1))
 
-        sn = keep.tile([P, NT, NH, S], F32)
-        m = keep.tile([P, NT, S], F32)
-        vcodes = keep.tile([P, NH * 2 * D], U32, align_bytes=64)
-        vscl = keep.tile([P, NH * 2 * D], U8, align_bytes=64)
-        ident_b = keep.tile([P, P], BF16)
-        ident_f = keep.tile([P, P], F32)
-        gn = keep.tile([P, 1], F32)
+        neg = keep.tile([P, Q_TILES, HEADS, SEQ], F32)
+        m = keep.tile([P, Q_TILES, SEQ], F32)
+        v_grouped = keep.tile([P, HEADS, PASSES, P, PACK], BF16, align_bytes=64)
+        v_codes = keep.tile([P, HEADS * WORDS], U32, align_bytes=64)
+        v_scales = keep.tile([P, HEADS * WORDS], U8, align_bytes=64)
+        ident_bf16 = keep.tile([P, P], BF16)
+        ident_f32 = keep.tile([P, P], F32)
+        neg_max = keep.tile([P, 1], F32)
         zero = keep.tile([P, 1], F32)
-        warm = keep.tile([P, 1], F32)
+        unused = keep.tile([P, 1], F32)
 
-        make_identity(nc, ident_b[:])
-        make_identity(nc, ident_f[:])
+        make_identity(nc, ident_bf16[:])
+        make_identity(nc, ident_f32[:])
         nc.vector.memset(zero[:], 0.0)
-        nc.scalar.activation(out=warm[:], in_=zero[:], func=ACT.Exp)
+        nc.scalar.activation(out=unused[:], in_=zero[:], func=ACT.Exp)
 
-        with ExitStack() as c1:
-            p1 = c1.enter_context(tc.tile_pool(name="p1", bufs=1))
-            ps_a = c1.enter_context(tc.psum_pool(name="ps_a", bufs=4))
-            ps_v = c1.enter_context(tc.psum_pool(name="ps_v", bufs=2))
-            q_sb = p1.tile([P, NH, S], BF16)
-            k_sb = p1.tile([P, NH, S], BF16)
-            v_sb = p1.tile([P, NH, S], BF16)
-            mk = p1.tile([P, NT, S], BF16)
-            gv = p1.tile([P, NH, 2, D, 4], BF16, align_bytes=64)
-            rm0 = p1.tile([P, S], F32)
-            rm1 = p1.tile([P, S], F32)
-            gp = p1.tile([P, 1], F32)
-            gb = p1.tile([P, P], F32)
-            rms = [rm0, rm1]
-            nc.vector.memset(rm0[:], -3.0e38)
-            nc.vector.memset(rm1[:], -3.0e38)
+        def quantise_v(head):
+            words = slice(head * WORDS, (head + 1) * WORDS)
+            nc.vector.quantize_mx(
+                out=v_codes[:, words].bitcast(FP8X4),
+                scales=v_scales[:, words],
+                in_=v_grouped[:, head].rearrange("p g d t -> p (g d t)"),
+            )
 
-            for n in range(NH):
-                nc.sync.dma_start(out=q_sb[:, n, :], in_=qv[:, n, :])
-                nc.sync.dma_start(out=k_sb[:, n, :], in_=kv[:, n, :])
-            nc.sync.dma_start(out=v_sb[:], in_=vv)
-            for t in range(0, NT, 2):
-                nc.sync.dma_start(out=mk[:, t : t + 2, :], in_=mv[:, t : t + 2, :])
+        with ExitStack() as part1:
+            loaded = part1.enter_context(tc.tile_pool(name="loaded", bufs=1))
+            score_banks = part1.enter_context(tc.psum_pool(name="score_banks", bufs=4))
+            v_banks = part1.enter_context(tc.psum_pool(name="v_banks", bufs=2))
+            max_bank = part1.enter_context(tc.psum_pool(name="max_bank", bufs=1))
+            q_sb = loaded.tile([P, HEADS, SEQ], BF16)
+            k_sb = loaded.tile([P, HEADS, SEQ], BF16)
+            v_sb = loaded.tile([P, HEADS, SEQ], BF16)
+            mask_sb = loaded.tile([P, Q_TILES, SEQ], BF16)
+            block_max = loaded.tile([P, BLOCKS - 1], F32)
+            earlier_max = loaded.tile([P, 1], F32)
+            last_max = [loaded.tile([P, 1], F32, name="last_max%d" % half) for half in range(2)]
+            spread = loaded.tile([P, P], F32)
 
-            for n in range(NH):
-                for it in range(NT):
-                    for jh in range(2):
-                        ps = ps_a.tile([P, HALF], F32)
+            first_q = 2 * P
+            nc.sync.dma_start(out=q_sb[:, 0, 0:first_q], in_=q_dram[:, 0, 0:first_q])
+            nc.sync.dma_start(out=k_sb[:, 0, 0:BANK], in_=k_dram[:, 0, 0:BANK])
+            nc.sync.dma_start(out=k_sb[:, 0, BANK:SEQ], in_=k_dram[:, 0, BANK:SEQ])
+            nc.sync.dma_start(out=q_sb[:, 0, first_q:SEQ], in_=q_dram[:, 0, first_q:SEQ])
+            for head in range(1, HEADS):
+                nc.sync.dma_start(out=q_sb[:, head, :], in_=q_dram[:, head, :])
+                nc.sync.dma_start(out=k_sb[:, head, :], in_=k_dram[:, head, :])
+            for t in range(0, Q_TILES, 2):
+                nc.sync.dma_start(out=mask_sb[:, t : t + 2, :], in_=mask_dram[:, t : t + 2, :])
+            nc.sync.dma_start(out=v_sb[:], in_=v_dram)
+
+            for t in range(Q_TILES):
+                nc.gpsimd.tensor_scalar(
+                    out=m[:, t, :], in0=mask_sb[:, t, :], scalar1=1.0e-4, scalar2=1.0,
+                    op0=ALU.mult, op1=ALU.add,
+                )
+
+            for head in range(HEADS):
+                for t in range(Q_TILES):
+                    block = head * Q_TILES + t
+                    for half in range(SEQ // BANK):
+                        keys = slice(half * BANK, (half + 1) * BANK)
+                        bank = score_banks.tile([P, BANK], F32)
                         nc.tensor.matmul(
-                            out=ps[:],
-                            lhsT=q_sb[:, n, it * P : (it + 1) * P],
-                            rhs=k_sb[:, n, jh * HALF : (jh + 1) * HALF],
-                            start=True,
-                            stop=True,
+                            out=bank[:], lhsT=q_sb[:, head, t * P : (t + 1) * P], rhs=k_sb[:, head, keys],
+                            start=True, stop=True,
                         )
-                        nc.scalar.activation(
-                            out=sn[:, it, n, jh * HALF : (jh + 1) * HALF],
-                            in_=ps[:],
-                            func=ACT.Copy,
-                            scale=-SCALE,
-                        )
-                    rm = rms[it % 2]
-                    nc.vector.tensor_tensor(out=rm[:], in0=sn[:, it, n, :], in1=rm[:], op=ALU.max)
-                    if n == 1:
-                        nc.vector.tensor_scalar(
-                            out=m[:, it, :],
-                            in0=mk[:, it, :],
-                            scalar1=1.0e-4,
-                            scalar2=1.0,
-                            op0=ALU.mult,
-                            op1=ALU.add,
-                        )
-                if n == 0:
-                    for h in range(NH):
-                        pv = ps_v.tile([P, S], BF16)
-                        for c in range(NT):
-                            nc.tensor.transpose(
-                                out=pv[:, c * P : (c + 1) * P],
-                                in_=v_sb[:, h, c * P : (c + 1) * P],
-                                identity=ident_b[:],
+                        nc.scalar.activation(out=neg[:, t, head, keys], in_=bank[:], func=ACT.Copy, scale=-SCALE)
+                        if block == BLOCKS - 1:
+                            nc.vector.tensor_reduce(
+                                out=last_max[half][:], in_=neg[:, t, head, keys], axis=AX.X, op=ALU.max
                             )
-                        nc.scalar.copy(
-                            out=gv[:, h],
-                            in_=pv[:].rearrange("p (g t d) -> p g d t", g=2, t=4),
+                    if block < BLOCKS - 1:
+                        nc.vector.tensor_reduce(
+                            out=block_max[:, block : block + 1], in_=neg[:, t, head, :], axis=AX.X, op=ALU.max
                         )
-                if n == 2:
-                    nc.vector.quantize_mx(
-                        out=vcodes[:].bitcast(FP8X4),
-                        scales=vscl[:],
-                        in_=gv[:].rearrange("p h g d t -> p (h g d t)"),
+                    if block == BLOCKS - 2:
+                        nc.vector.tensor_reduce(out=earlier_max[:], in_=block_max[:], axis=AX.X, op=ALU.max)
+
+            v_bank = {}
+
+            def transpose_v(head):
+                v_bank[head] = v_banks.tile([P, SEQ], BF16, name="v_bank")
+                for c in range(CHUNKS):
+                    nc.tensor.transpose(
+                        out=v_bank[head][:, c * P : (c + 1) * P], in_=v_sb[:, head, c * P : (c + 1) * P],
+                        identity=ident_bf16[:],
                     )
 
-            nc.vector.tensor_tensor(out=rm0[:], in0=rm0[:], in1=rm1[:], op=ALU.max)
-            nc.vector.tensor_reduce(out=gp[:], in_=rm0[:], axis=AX.X, op=ALU.max)
-            nc.vector.tensor_copy(out=gb[:], in_=gp[:, 0:1].to_broadcast([P, P]))
-            pg = ps_g.tile([P, P], F32)
-            nc.tensor.transpose(out=pg[:], in_=gb[:], identity=ident_f[:])
-            nc.vector.tensor_reduce(out=gn[:], in_=pg[:], axis=AX.X, op=ALU.max)
+            def regroup_v(head):
+                nc.scalar.copy(
+                    out=v_grouped[:, head],
+                    in_=v_bank[head][:].rearrange("p (g t d) -> p g d t", g=PASSES, t=PACK),
+                )
+
+            transpose_v(0)
+            transpose_v(1)
+            nc.vector.tensor_scalar(
+                out=spread[:], in0=last_max[1][:, 0:1].to_broadcast([P, P]),
+                scalar1=last_max[0][:, 0:1], scalar2=earlier_max[:, 0:1], op0=ALU.max, op1=ALU.max,
+            )
+            spread_t = max_bank.tile([P, P], F32)
+            nc.tensor.transpose(out=spread_t[:], in_=spread[:], identity=ident_f32[:])
+            regroup_v(0)
+            regroup_v(1)
+            transpose_v(2)
+            transpose_v(3)
+            regroup_v(2)
+            regroup_v(3)
+            quantise_v(0)
+            nc.vector.tensor_reduce(out=neg_max[:], in_=spread_t[:], axis=AX.X, op=ALU.max)
 
         work = ctx.enter_context(tc.tile_pool(name="work", bufs=3))
-        stat = ctx.enter_context(tc.tile_pool(name="stat", bufs=4))
-        ps_t = ctx.enter_context(tc.psum_pool(name="ps_t", bufs=3))
-        ps_o = ctx.enter_context(tc.psum_pool(name="ps_o", bufs=2))
-        NB = NT * NH
-        st = {}
+        stats = ctx.enter_context(tc.tile_pool(name="stats", bufs=4))
+        attn_banks = ctx.enter_context(tc.psum_pool(name="attn_banks", bufs=3))
+        out_banks = ctx.enter_context(tc.psum_pool(name="out_banks", bufs=2))
+        live = {}
 
-        def row(rb):
-            return sn[:, rb // NH, rb % NH, :]
+        def row(b):
+            return neg[:, b // HEADS, b % HEADS, :]
 
-        def stage_a(rb):
+        def blend(b):
             nc.vector.scalar_tensor_tensor(
-                out=row(rb), in0=row(rb), scalar=gn[:, 0:1], in1=m[:, rb // NH, :],
+                out=row(b), in0=row(b), scalar=neg_max[:, 0:1], in1=m[:, b // HEADS, :],
                 op0=ALU.subtract, op1=ALU.mult,
             )
-            nb = stat.tile([P, 1], F32)
-            nc.vector.tensor_reduce(out=nb[:], in_=row(rb), axis=AX.X, op=ALU.min)
-            nc.scalar.activation(out=row(rb), in_=row(rb), func=ACT.Exp, bias=nb[:, 0:1], scale=-1.0)
 
-        def stage_c(rb):
-            z = stat.tile([P, 1], F32)
+        def row_max(b):
+            live["bias", b] = stats.tile([P, 1], F32, name="bias")
+            nc.vector.tensor_reduce(out=live["bias", b][:], in_=row(b), axis=AX.X, op=ALU.min)
+
+        def exponential(b):
+            nc.scalar.activation(out=row(b), in_=row(b), func=ACT.Exp, bias=live["bias", b][:, 0:1], scale=-1.0)
+
+        def weigh(b):
+            live["sum", b] = stats.tile([P, 1], F32, name="sum")
             nc.vector.scalar_tensor_tensor(
-                out=row(rb), in0=row(rb), scalar=1.0, in1=m[:, rb // NH, :],
-                op0=ALU.mult, op1=ALU.mult, accum_out=z[:],
+                out=row(b), in0=row(b), scalar=1.0, in1=m[:, b // HEADS, :],
+                op0=ALU.mult, op1=ALU.mult, accum_out=live["sum", b][:],
             )
-            r = stat.tile([P, 1], F32)
-            nc.vector.reciprocal(out=r[:], in_=z[:])
-            at = work.tile([P, S], BF16)
-            nc.scalar.activation(out=at[:], in_=row(rb), func=ACT.Copy, scale=r[:, 0:1])
-            pt = ps_t.tile([P, S], BF16)
-            for c in range(NT):
+
+        def reciprocal(b):
+            live["inv", b] = stats.tile([P, 1], F32, name="inv")
+            nc.vector.reciprocal(out=live["inv", b][:], in_=live["sum", b][:])
+
+        def normalise(b):
+            live["attn", b] = work.tile([P, SEQ], BF16, name="attn")
+            nc.scalar.activation(out=live["attn", b][:], in_=row(b), func=ACT.Copy, scale=live["inv", b][:, 0:1])
+
+        def transpose(b):
+            live["attn_t", b] = attn_banks.tile([P, SEQ], BF16, name="attn_t")
+            for c in range(CHUNKS):
                 nc.tensor.transpose(
-                    out=pt[:, c * P : (c + 1) * P], in_=at[:, c * P : (c + 1) * P], identity=ident_b[:]
+                    out=live["attn_t", b][:, c * P : (c + 1) * P], in_=live["attn", b][:, c * P : (c + 1) * P],
+                    identity=ident_bf16[:],
                 )
-            st[("pt", rb)] = pt
 
-        def stage_f(rb):
-            pt = st[("pt", rb)]
-            gr = work.tile([P, S], BF16, align_bytes=64)
-            nc.scalar.copy(
-                out=gr[:].rearrange("p (g i t) -> p g i t", g=2, t=4),
-                in_=pt[:].rearrange("p (g t i) -> p g i t", g=2, t=4),
+        def regroup(b, engine_copy):
+            live["grouped", b] = work.tile([P, SEQ], BF16, name="grouped", align_bytes=64)
+            engine_copy(
+                out=live["grouped", b][:].rearrange("p (g i t) -> p g i t", g=PASSES, t=PACK),
+                in_=live["attn_t", b][:].rearrange("p (g t i) -> p g i t", g=PASSES, t=PACK),
             )
-            st[("gr", rb)] = gr
 
-        def stage_g(rb):
-            it, n = rb // NH, rb % NH
-            gr = st[("gr", rb)]
-            cd = work.tile([P, 2 * P], U32, align_bytes=64)
-            sc = work.tile([P, 2 * P], U8, align_bytes=64)
-            nc.vector.quantize_mx(out=cd[:].bitcast(FP8X4), scales=sc[:], in_=gr[:])
-            if n == 0:
-                po_new = ps_o.tile([P, NH * P], F32)
-                st["po"] = po_new
-            po = st["po"]
-            for g in range(2):
-                w = (n * 2 + g) * D
+        def quantise(b):
+            live["codes", b] = work.tile([P, WORDS], U32, name="codes", align_bytes=64)
+            live["scales", b] = work.tile([P, WORDS], U8, name="scales", align_bytes=64)
+            nc.vector.quantize_mx(
+                out=live["codes", b][:].bitcast(FP8X4), scales=live["scales", b][:], in_=live["grouped", b][:]
+            )
+
+        def multiply(b):
+            head = b % HEADS
+            if head == 0:
+                live["out", b // HEADS] = out_banks.tile([P, HEADS * P], F32, name="out_bank")
+            for g in range(PASSES):
+                v_words = slice(head * WORDS + g * P, head * WORDS + (g + 1) * P)
+                a_words = slice(g * P, (g + 1) * P)
                 nc.tensor.matmul_mx(
-                    out=po[:, n * P : (n + 1) * P],
-                    lhsT=vcodes[:, w : w + D].bitcast(FP8X4),
-                    lhsT_scale=vscl[:, w : w + D],
-                    rhs=cd[:, g * P : (g + 1) * P].bitcast(FP8X4),
-                    rhs_scale=sc[:, g * P : (g + 1) * P],
-                    start=(g == 0),
-                    stop=(g == 1),
-                )
-            if n == NH - 1:
-                ob = work.tile([P, NH * P], F32)
-                nc.scalar.copy(out=ob[:], in_=po[:])
-                nc.sync.dma_start(
-                    out=ov[:, :, it * P : (it + 1) * P],
-                    in_=ob[:].rearrange("p (n i) -> p n i", n=NH),
+                    out=live["out", b // HEADS][:, head * P : (head + 1) * P],
+                    lhsT=v_codes[:, v_words].bitcast(FP8X4), lhsT_scale=v_scales[:, v_words],
+                    rhs=live["codes", b][:, a_words].bitcast(FP8X4), rhs_scale=live["scales", b][:, a_words],
+                    start=(g == 0), stop=(g == PASSES - 1),
                 )
 
-        for i in range(NB + 3):
-            if i < NB:
-                stage_a(i)
-            if 0 <= i - 1 < NB:
-                stage_c(i - 1)
-            if 0 <= i - 2 < NB:
-                stage_f(i - 2)
-            if 0 <= i - 3 < NB:
-                stage_g(i - 3)
+        def store(t):
+            out_sb = work.tile([P, HEADS * P], F32)
+            nc.scalar.copy(out=out_sb[:], in_=live["out", t][:])
+            nc.sync.dma_start(
+                out=out_dram[:, :, t * P : (t + 1) * P], in_=out_sb[:].rearrange("p (n i) -> p n i", n=HEADS)
+            )
+
+        def stage(lag, i, fn, *args):
+            if 0 <= i - lag < BLOCKS:
+                fn(i - lag, *args)
+
+        for i in range(BLOCKS + 7):
+            stage(0, i, blend)
+            stage(2, i, weigh)
+            stage(0, i, row_max)
+            stage(2, i, reciprocal)
+            if i + 1 < HEADS:
+                quantise_v(i + 1)
+            stage(1, i, exponential)
+            stage(3, i, normalise)
+            stage(3, i, transpose)
+            stage(4, i, regroup, nc.scalar.copy if i < BLOCKS else nc.vector.tensor_copy)
+            stage(5, i, quantise)
+            stage(5, i, multiply)
+            if 0 <= i - 6 < BLOCKS and (i - 6) % HEADS == HEADS - 1:
+                store((i - 6) // HEADS)

@@ -224,7 +224,7 @@ def tile_mhattention_own_kernel(tc, q, k, v, attn_mask, out):
 
         def store(t):
             out_sb = work.tile([P, HEADS * P], F32)
-            nc.scalar.copy(out=out_sb[:], in_=live["out", t][:])
+            nc.vector.tensor_copy(out=out_sb[:], in_=live["out", t][:])
             nc.sync.dma_start(
                 out=out_dram[:, :, t * P : (t + 1) * P], in_=out_sb[:].rearrange("p (n i) -> p n i", n=HEADS)
             )

@@ -16,14 +16,21 @@ P = 128
 HEADS = 4
 SEQ = 1024
 Q_TILES = SEQ // P
+ROW_BLOCKS = Q_TILES * HEADS
 CHUNKS = SEQ // P
 BANK = 512
 PACK = 4
 PASSES = SEQ // (P * PACK)
 WORDS = PASSES * P
-BLOCKS = Q_TILES * HEADS
 SCALE = P ** -0.5
 FLOPS = 2 * 2 * HEADS * SEQ * SEQ * P
+
+LAG_EXP = 1
+LAG_WEIGH = 2
+LAG_NORMALISE = 3
+LAG_REGROUP = 4
+LAG_QUANTISE = 5
+LAG_STORE = 6
 
 
 def tile_mhattention_own_kernel(tc, q, k, v, attn_mask, out):
@@ -32,7 +39,7 @@ def tile_mhattention_own_kernel(tc, q, k, v, attn_mask, out):
     k_dram = k.rearrange("b c h w -> (b c) (h w)").rearrange("(n d) s -> d n s", d=P)
     v_dram = v.rearrange("b c h w -> (b c) (h w)").rearrange("(n d) s -> d n s", d=P)
     out_dram = out.rearrange("b c h w -> (b c) (h w)").rearrange("(n d) s -> d n s", d=P)
-    mask_dram = attn_mask.rearrange("b i j -> (b i) j").rearrange("(t p) j -> p t j", p=P)
+    mask_dram = attn_mask.rearrange("b i j -> (b i) j").rearrange("(qt p) j -> p qt j", p=P)
 
     with ExitStack() as ctx:
         ctx.enter_context(tc.manual_schedule())
@@ -47,19 +54,19 @@ def tile_mhattention_own_kernel(tc, q, k, v, attn_mask, out):
         ident_f32 = keep.tile([P, P], F32)
         neg_max = keep.tile([P, 1], F32)
         zero = keep.tile([P, 1], F32)
-        unused = keep.tile([P, 1], F32)
+        exp_of_zero = keep.tile([P, 1], F32)
 
         make_identity(nc, ident_bf16[:])
         make_identity(nc, ident_f32[:])
         nc.vector.memset(zero[:], 0.0)
-        nc.scalar.activation(out=unused[:], in_=zero[:], func=ACT.Exp)
+        nc.scalar.activation(out=exp_of_zero[:], in_=zero[:], func=ACT.Exp)
 
         def quantise_v(head):
             words = slice(head * WORDS, (head + 1) * WORDS)
             nc.vector.quantize_mx(
                 out=v_codes[:, words].bitcast(FP8X4),
                 scales=v_scales[:, words],
-                in_=v_grouped[:, head].rearrange("p g d t -> p (g d t)"),
+                in_=v_grouped[:, head].rearrange("p ps d t -> p (ps d t)"),
             )
 
         with ExitStack() as part1:
@@ -71,7 +78,7 @@ def tile_mhattention_own_kernel(tc, q, k, v, attn_mask, out):
             k_sb = loaded.tile([P, HEADS, SEQ], BF16)
             v_sb = loaded.tile([P, HEADS, SEQ], BF16)
             mask_sb = loaded.tile([P, Q_TILES, SEQ], BF16)
-            block_max = loaded.tile([P, BLOCKS - 1], F32)
+            block_max = loaded.tile([P, ROW_BLOCKS - 1], F32)
             earlier_max = loaded.tile([P, 1], F32)
             last_max = [loaded.tile([P, 1], F32, name="last_max%d" % half) for half in range(2)]
             spread = loaded.tile([P, P], F32)
@@ -84,36 +91,36 @@ def tile_mhattention_own_kernel(tc, q, k, v, attn_mask, out):
             for head in range(1, HEADS):
                 nc.sync.dma_start(out=q_sb[:, head, :], in_=q_dram[:, head, :])
                 nc.sync.dma_start(out=k_sb[:, head, :], in_=k_dram[:, head, :])
-            for t in range(0, Q_TILES, 2):
-                nc.sync.dma_start(out=mask_sb[:, t : t + 2, :], in_=mask_dram[:, t : t + 2, :])
+            for qt in range(0, Q_TILES, 2):
+                nc.sync.dma_start(out=mask_sb[:, qt : qt + 2, :], in_=mask_dram[:, qt : qt + 2, :])
             nc.sync.dma_start(out=v_sb[:], in_=v_dram)
 
-            for t in range(Q_TILES):
+            for qt in range(Q_TILES):
                 nc.gpsimd.tensor_scalar(
-                    out=m[:, t, :], in0=mask_sb[:, t, :], scalar1=1.0e-4, scalar2=1.0,
+                    out=m[:, qt, :], in0=mask_sb[:, qt, :], scalar1=1.0e-4, scalar2=1.0,
                     op0=ALU.mult, op1=ALU.add,
                 )
 
             for head in range(HEADS):
-                for t in range(Q_TILES):
-                    block = head * Q_TILES + t
+                for qt in range(Q_TILES):
+                    done = head * Q_TILES + qt
                     for half in range(SEQ // BANK):
                         keys = slice(half * BANK, (half + 1) * BANK)
                         bank = score_banks.tile([P, BANK], F32)
                         nc.tensor.matmul(
-                            out=bank[:], lhsT=q_sb[:, head, t * P : (t + 1) * P], rhs=k_sb[:, head, keys],
+                            out=bank[:], lhsT=q_sb[:, head, qt * P : (qt + 1) * P], rhs=k_sb[:, head, keys],
                             start=True, stop=True,
                         )
-                        nc.scalar.activation(out=neg[:, t, head, keys], in_=bank[:], func=ACT.Copy, scale=-SCALE)
-                        if block == BLOCKS - 1:
+                        nc.scalar.activation(out=neg[:, qt, head, keys], in_=bank[:], func=ACT.Copy, scale=-SCALE)
+                        if done == ROW_BLOCKS - 1:
                             nc.vector.tensor_reduce(
-                                out=last_max[half][:], in_=neg[:, t, head, keys], axis=AX.X, op=ALU.max
+                                out=last_max[half][:], in_=neg[:, qt, head, keys], axis=AX.X, op=ALU.max
                             )
-                    if block < BLOCKS - 1:
+                    if done < ROW_BLOCKS - 1:
                         nc.vector.tensor_reduce(
-                            out=block_max[:, block : block + 1], in_=neg[:, t, head, :], axis=AX.X, op=ALU.max
+                            out=block_max[:, done : done + 1], in_=neg[:, qt, head, :], axis=AX.X, op=ALU.max
                         )
-                    if block == BLOCKS - 2:
+                    if done == ROW_BLOCKS - 2:
                         nc.vector.tensor_reduce(out=earlier_max[:], in_=block_max[:], axis=AX.X, op=ALU.max)
 
             v_bank = {}
@@ -129,7 +136,7 @@ def tile_mhattention_own_kernel(tc, q, k, v, attn_mask, out):
             def regroup_v(head):
                 nc.scalar.copy(
                     out=v_grouped[:, head],
-                    in_=v_bank[head][:].rearrange("p (g t d) -> p g d t", g=PASSES, t=PACK),
+                    in_=v_bank[head][:].rearrange("p (ps t d) -> p ps d t", ps=PASSES, t=PACK),
                 )
 
             transpose_v(0)
@@ -194,11 +201,11 @@ def tile_mhattention_own_kernel(tc, q, k, v, attn_mask, out):
                     identity=ident_bf16[:],
                 )
 
-        def regroup(b, engine_copy):
+        def regroup(b, copy):
             live["grouped", b] = work.tile([P, SEQ], BF16, name="grouped", align_bytes=64)
-            engine_copy(
-                out=live["grouped", b][:].rearrange("p (g i t) -> p g i t", g=PASSES, t=PACK),
-                in_=live["attn_t", b][:].rearrange("p (g t i) -> p g i t", g=PASSES, t=PACK),
+            copy(
+                out=live["grouped", b][:].rearrange("p (ps i t) -> p ps i t", ps=PASSES, t=PACK),
+                in_=live["attn_t", b][:].rearrange("p (ps t i) -> p ps i t", ps=PASSES, t=PACK),
             )
 
         def quantise(b):
@@ -212,39 +219,41 @@ def tile_mhattention_own_kernel(tc, q, k, v, attn_mask, out):
             head = b % HEADS
             if head == 0:
                 live["out", b // HEADS] = out_banks.tile([P, HEADS * P], F32, name="out_bank")
-            for g in range(PASSES):
-                v_words = slice(head * WORDS + g * P, head * WORDS + (g + 1) * P)
-                a_words = slice(g * P, (g + 1) * P)
+            for ps in range(PASSES):
+                v_words = slice(head * WORDS + ps * P, head * WORDS + (ps + 1) * P)
+                attn_words = slice(ps * P, (ps + 1) * P)
                 nc.tensor.matmul_mx(
                     out=live["out", b // HEADS][:, head * P : (head + 1) * P],
                     lhsT=v_codes[:, v_words].bitcast(FP8X4), lhsT_scale=v_scales[:, v_words],
-                    rhs=live["codes", b][:, a_words].bitcast(FP8X4), rhs_scale=live["scales", b][:, a_words],
-                    start=(g == 0), stop=(g == PASSES - 1),
+                    rhs=live["codes", b][:, attn_words].bitcast(FP8X4),
+                    rhs_scale=live["scales", b][:, attn_words],
+                    start=(ps == 0), stop=(ps == PASSES - 1),
                 )
 
-        def store(t):
-            out_sb = work.tile([P, HEADS * P], F32)
-            nc.vector.tensor_copy(out=out_sb[:], in_=live["out", t][:])
-            nc.sync.dma_start(
-                out=out_dram[:, :, t * P : (t + 1) * P], in_=out_sb[:].rearrange("p (n i) -> p n i", n=HEADS)
-            )
+        def store(b):
+            if b % HEADS == HEADS - 1:
+                qt = b // HEADS
+                out_sb = work.tile([P, HEADS * P], F32)
+                nc.scalar.copy(out=out_sb[:], in_=live["out", qt][:])
+                nc.sync.dma_start(
+                    out=out_dram[:, :, qt * P : (qt + 1) * P], in_=out_sb[:].rearrange("p (n i) -> p n i", n=HEADS)
+                )
 
-        def stage(lag, i, fn, *args):
-            if 0 <= i - lag < BLOCKS:
-                fn(i - lag, *args)
+        def stage(i, lag, work_on, *args):
+            if 0 <= i - lag < ROW_BLOCKS:
+                work_on(i - lag, *args)
 
-        for i in range(BLOCKS + 7):
-            stage(0, i, blend)
-            stage(2, i, weigh)
-            stage(0, i, row_max)
-            stage(2, i, reciprocal)
+        for i in range(ROW_BLOCKS + LAG_STORE + 1):
+            stage(i, 0, blend)
+            stage(i, LAG_WEIGH, weigh)
+            stage(i, 0, row_max)
+            stage(i, LAG_WEIGH, reciprocal)
             if i + 1 < HEADS:
                 quantise_v(i + 1)
-            stage(1, i, exponential)
-            stage(3, i, normalise)
-            stage(3, i, transpose)
-            stage(4, i, regroup, nc.scalar.copy if i < BLOCKS else nc.vector.tensor_copy)
-            stage(5, i, quantise)
-            stage(5, i, multiply)
-            if 0 <= i - 6 < BLOCKS and (i - 6) % HEADS == HEADS - 1:
-                store((i - 6) // HEADS)
+            stage(i, LAG_EXP, exponential)
+            stage(i, LAG_NORMALISE, normalise)
+            stage(i, LAG_NORMALISE, transpose)
+            stage(i, LAG_REGROUP, regroup, nc.scalar.copy if i < ROW_BLOCKS else nc.vector.tensor_copy)
+            stage(i, LAG_QUANTISE, quantise)
+            stage(i, LAG_QUANTISE, multiply)
+            stage(i, LAG_STORE, store)

@@ -19,18 +19,15 @@ Q_TILES = SEQ // P
 ROW_BLOCKS = Q_TILES * HEADS
 CHUNKS = SEQ // P
 BANK = 512
+HALVES = SEQ // BANK
+Q_HALF = BANK // P
 PACK = 4
 PASSES = SEQ // (P * PACK)
 WORDS = PASSES * P
 SCALE = P ** -0.5
 FLOPS = 2 * 2 * HEADS * SEQ * SEQ * P
 
-LAG_EXP = 1
-LAG_WEIGH = 2
-LAG_NORMALISE = 3
-LAG_REGROUP = 4
-LAG_QUANTISE = 5
-LAG_STORE = 6
+GPSIMD_BLOCKS = 16
 
 
 def tile_mhattention_own_kernel(tc, q, k, v, attn_mask, out):
@@ -45,144 +42,230 @@ def tile_mhattention_own_kernel(tc, q, k, v, attn_mask, out):
         ctx.enter_context(tc.manual_schedule())
         keep = ctx.enter_context(tc.tile_pool(name="keep", bufs=1))
 
-        neg = keep.tile([P, Q_TILES, HEADS, SEQ], F32)
-        m = keep.tile([P, Q_TILES, SEQ], F32)
-        v_grouped = keep.tile([P, HEADS, PASSES, P, PACK], BF16, align_bytes=64)
+        scores = keep.tile([P, HALVES, HEADS, Q_HALF, CHUNKS, P], F32)
+        m_t = keep.tile([P, Q_TILES, CHUNKS, P], F32)
+        add_t = keep.tile([P, Q_TILES, CHUNKS, P], F32)
         v_codes = keep.tile([P, HEADS * WORDS], U32, align_bytes=64)
         v_scales = keep.tile([P, HEADS * WORDS], U8, align_bytes=64)
         ident_bf16 = keep.tile([P, P], BF16)
         ident_f32 = keep.tile([P, P], F32)
-        neg_max = keep.tile([P, 1], F32)
-        zero = keep.tile([P, 1], F32)
-        exp_of_zero = keep.tile([P, 1], F32)
+        minus_g = keep.tile([P, 1], F32)
+        one = keep.tile([P, 1], F32)
+        ln_of_one = keep.tile([P, 1], F32)
 
+        nc.vector.memset(one[:], 1.0)
+        nc.scalar.activation(out=ln_of_one[:], in_=one[:], func=ACT.Ln)
         make_identity(nc, ident_bf16[:])
         make_identity(nc, ident_f32[:])
-        nc.vector.memset(zero[:], 0.0)
-        nc.scalar.activation(out=exp_of_zero[:], in_=zero[:], func=ACT.Exp)
+
+        def block(b):
+            qt, head = b // HEADS, b % HEADS
+            return scores[:, qt // Q_HALF, head, qt % Q_HALF].rearrange("p c i -> p (c i)")
+
+        def m_of(qt):
+            return m_t[:, qt].rearrange("p c i -> p (c i)")
+
+        def add_of(qt):
+            return add_t[:, qt].rearrange("p c i -> p (c i)")
+
+        def weigh_gpsimd(b):
+            nc.gpsimd.tensor_tensor(out=block(b), in0=block(b), in1=m_of(b // HEADS), op=ALU.mult)
+
+        def weigh_vector(b):
+            nc.vector.tensor_tensor(out=block(b), in0=block(b), in1=m_of(b // HEADS), op=ALU.mult)
 
         def quantise_v(head):
             words = slice(head * WORDS, (head + 1) * WORDS)
             nc.vector.quantize_mx(
                 out=v_codes[:, words].bitcast(FP8X4),
                 scales=v_scales[:, words],
-                in_=v_grouped[:, head].rearrange("p ps d t -> p (ps d t)"),
+                in_=v_grouped[head][:],
             )
+
+        v_grouped = {}
+        v_pool = ctx.enter_context(tc.tile_pool(name="v_pool", bufs=2))
 
         with ExitStack() as part1:
             loaded = part1.enter_context(tc.tile_pool(name="loaded", bufs=1))
-            score_banks = part1.enter_context(tc.psum_pool(name="score_banks", bufs=4))
-            v_banks = part1.enter_context(tc.psum_pool(name="v_banks", bufs=2))
+            mask_pool = part1.enter_context(tc.tile_pool(name="masks", bufs=4))
+            score_banks = part1.enter_context(tc.psum_pool(name="score_banks", bufs=5))
+            turned_banks = part1.enter_context(tc.psum_pool(name="turned_banks", bufs=2))
             max_bank = part1.enter_context(tc.psum_pool(name="max_bank", bufs=1))
             q_sb = loaded.tile([P, HEADS, SEQ], BF16)
             k_sb = loaded.tile([P, HEADS, SEQ], BF16)
             v_sb = loaded.tile([P, HEADS, SEQ], BF16)
-            mask_sb = loaded.tile([P, Q_TILES, SEQ], BF16)
-            block_max = loaded.tile([P, ROW_BLOCKS - 1], F32)
-            earlier_max = loaded.tile([P, 1], F32)
-            last_max = [loaded.tile([P, 1], F32, name="last_max%d" % half) for half in range(2)]
+            PAIRS = HALVES * HEADS * CHUNKS // 2
+            mins = loaded.tile([P, PAIRS + PAIRS // 2], F32)
+            earlier_min = loaded.tile([P, 1], F32)
+            last_min = loaded.tile([P, 1], F32)
             spread = loaded.tile([P, P], F32)
+            mask_sb = {}
 
-            first_q = 2 * P
-            nc.sync.dma_start(out=q_sb[:, 0, 0:first_q], in_=q_dram[:, 0, 0:first_q])
-            nc.sync.dma_start(out=k_sb[:, 0, 0:BANK], in_=k_dram[:, 0, 0:BANK])
-            nc.sync.dma_start(out=k_sb[:, 0, BANK:SEQ], in_=k_dram[:, 0, BANK:SEQ])
-            nc.sync.dma_start(out=q_sb[:, 0, first_q:SEQ], in_=q_dram[:, 0, first_q:SEQ])
+            def load_mask(qt):
+                mask_sb[qt] = mask_pool.tile([P, SEQ], BF16, name="mask_sb")
+                nc.sync.dma_start(out=mask_sb[qt][:], in_=mask_dram[:, qt, :])
+
+            first_k = 2 * P
+            nc.sync.dma_start(out=k_sb[:, 0, 0:first_k], in_=k_dram[:, 0, 0:first_k])
+            nc.sync.dma_start(out=q_sb[:, 0, 0:BANK], in_=q_dram[:, 0, 0:BANK])
+            nc.sync.dma_start(out=k_sb[:, 0, first_k:SEQ], in_=k_dram[:, 0, first_k:SEQ])
+            load_mask(0)
+            load_mask(1)
             for head in range(1, HEADS):
-                nc.sync.dma_start(out=q_sb[:, head, :], in_=q_dram[:, head, :])
+                nc.sync.dma_start(out=q_sb[:, head, 0:BANK], in_=q_dram[:, head, 0:BANK])
                 nc.sync.dma_start(out=k_sb[:, head, :], in_=k_dram[:, head, :])
-            for qt in range(0, Q_TILES, 2):
-                nc.sync.dma_start(out=mask_sb[:, qt : qt + 2, :], in_=mask_dram[:, qt : qt + 2, :])
+                if head < 3:
+                    load_mask(head + 1)
+            nc.sync.dma_start(out=q_sb[:, :, BANK:SEQ], in_=q_dram[:, :, BANK:SEQ])
+            for qt in range(4, Q_TILES):
+                load_mask(qt)
             nc.sync.dma_start(out=v_sb[:], in_=v_dram)
 
-            for qt in range(Q_TILES):
-                nc.gpsimd.tensor_scalar(
-                    out=m[:, qt, :], in0=mask_sb[:, qt, :], scalar1=1.0e-4, scalar2=1.0,
-                    op0=ALU.mult, op1=ALU.add,
-                )
-
-            for head in range(HEADS):
-                for qt in range(Q_TILES):
-                    done = head * Q_TILES + qt
-                    for half in range(SEQ // BANK):
-                        keys = slice(half * BANK, (half + 1) * BANK)
-                        bank = score_banks.tile([P, BANK], F32)
-                        nc.tensor.matmul(
-                            out=bank[:], lhsT=q_sb[:, head, qt * P : (qt + 1) * P], rhs=k_sb[:, head, keys],
-                            start=True, stop=True,
-                        )
-                        nc.scalar.activation(out=neg[:, qt, head, keys], in_=bank[:], func=ACT.Copy, scale=-SCALE)
-                        if done == ROW_BLOCKS - 1:
-                            nc.vector.tensor_reduce(
-                                out=last_max[half][:], in_=neg[:, qt, head, keys], axis=AX.X, op=ALU.max
-                            )
-                    if done < ROW_BLOCKS - 1:
-                        nc.vector.tensor_reduce(
-                            out=block_max[:, done : done + 1], in_=neg[:, qt, head, :], axis=AX.X, op=ALU.max
-                        )
-                    if done == ROW_BLOCKS - 2:
-                        nc.vector.tensor_reduce(out=earlier_max[:], in_=block_max[:], axis=AX.X, op=ALU.max)
-
-            v_bank = {}
-
-            def transpose_v(head):
-                v_bank[head] = v_banks.tile([P, SEQ], BF16, name="v_bank")
+            def turn(source):
+                bank = turned_banks.tile([P, SEQ], BF16, name="turned")
                 for c in range(CHUNKS):
                     nc.tensor.transpose(
-                        out=v_bank[head][:, c * P : (c + 1) * P], in_=v_sb[:, head, c * P : (c + 1) * P],
-                        identity=ident_bf16[:],
+                        out=bank[:, c * P : (c + 1) * P], in_=source[:, c * P : (c + 1) * P], identity=ident_bf16[:]
                     )
+                return bank
 
-            def regroup_v(head):
+            def make_m(qt):
+                bank = turn(mask_sb[qt][:])
+                nc.scalar.activation(out=m_of(qt), in_=bank[:], func=ACT.Copy, scale=1.0e-4, bias=1.0)
+
+            def make_ln(qt):
+                nc.scalar.activation(out=add_of(qt), in_=m_of(qt), func=ACT.Ln)
+
+            side_work = [(make_m, qt) for qt in range(Q_TILES)] + [(make_ln, qt) for qt in range(Q_TILES)]
+            made_m, heads_done, to_weigh = [], [], [(t, head) for head in range(HEADS) for t in range(Q_HALF)]
+            n_mins = 0
+            pending = None
+            pair = 0
+            for half in range(HALVES):
+                queries = slice(half * BANK, (half + 1) * BANK)
+                for head in range(HEADS):
+                    for pr in range(CHUNKS // 2):
+                        last = pair == PAIRS - 1
+                        for c in (2 * pr, 2 * pr + 1):
+                            bank = score_banks.tile([P, BANK], F32, name="bank")
+                            nc.tensor.matmul(
+                                out=bank[:], lhsT=k_sb[:, head, c * P : (c + 1) * P], rhs=q_sb[:, head, queries],
+                                start=True, stop=True,
+                            )
+                            place = scores[:, half, head, :, c, :]
+                            bank_view = bank[:].rearrange("p (t i) -> p t i", t=Q_HALF)
+                            if pr % 2 == 0:
+                                nc.scalar.activation(out=place, in_=bank_view, func=ACT.Copy, scale=SCALE)
+                            else:
+                                if last and c == 2 * pr + 1:
+                                    nc.vector.tensor_reduce(
+                                        out=mins[:, n_mins : n_mins + 1], in_=pending, axis=AX.XY, op=ALU.min
+                                    )
+                                    n_mins += 1
+                                    column = last_min[:]
+                                else:
+                                    column = mins[:, n_mins : n_mins + 1]
+                                    n_mins += 1
+                                nc.vector.tensor_scalar(
+                                    out=place, in0=bank_view, scalar1=SCALE, scalar2=None,
+                                    op0=ALU.mult, op1=ALU.min, accum_out=column,
+                                )
+                        if pr % 2 == 0:
+                            pending = scores[:, half, head, :, 2 * pr : 2 * pr + 2, :].rearrange("p t c i -> p t (c i)")
+                            if side_work:
+                                work_on, qt = side_work.pop(0)
+                                work_on(qt)
+                                if work_on == make_m:
+                                    made_m.append(qt)
+                        elif not last:
+                            nc.vector.tensor_reduce(out=mins[:, n_mins : n_mins + 1], in_=pending, axis=AX.XY, op=ALU.min)
+                            n_mins += 1
+                        pair += 1
+                        if half == 0 and pr == CHUNKS // 2 - 1:
+                            heads_done.append(head)
+                        while to_weigh and to_weigh[0][0] in made_m and to_weigh[0][1] in heads_done:
+                            t, done_head = to_weigh.pop(0)
+                            weigh_gpsimd(t * HEADS + done_head)
+            nc.vector.tensor_reduce(out=earlier_min[:], in_=mins[:, 0:n_mins], axis=AX.X, op=ALU.min)
+
+            def regroup_v(head, bank):
+                v_grouped[head] = v_pool.tile([P, PASSES * P * PACK], BF16, name="v_grouped", align_bytes=64)
                 nc.scalar.copy(
-                    out=v_grouped[:, head],
-                    in_=v_bank[head][:].rearrange("p (ps t d) -> p ps d t", ps=PASSES, t=PACK),
+                    out=v_grouped[head][:].rearrange("p (ps d t) -> p ps d t", ps=PASSES, t=PACK),
+                    in_=bank[:].rearrange("p (ps t d) -> p ps d t", ps=PASSES, t=PACK),
                 )
 
-            transpose_v(0)
-            transpose_v(1)
+            turned = [turn(v_sb[:, head, :]) for head in range(2)]
             nc.vector.tensor_scalar(
-                out=spread[:], in0=last_max[1][:, 0:1].to_broadcast([P, P]),
-                scalar1=last_max[0][:, 0:1], scalar2=earlier_max[:, 0:1], op0=ALU.max, op1=ALU.max,
+                out=spread[:], in0=last_min[:, 0:1].to_broadcast([P, P]),
+                scalar1=earlier_min[:, 0:1], scalar2=-1.0, op0=ALU.min, op1=ALU.mult,
             )
             spread_t = max_bank.tile([P, P], F32)
             nc.tensor.transpose(out=spread_t[:], in_=spread[:], identity=ident_f32[:])
-            regroup_v(0)
-            regroup_v(1)
-            transpose_v(2)
-            transpose_v(3)
-            regroup_v(2)
-            regroup_v(3)
+            regroup_v(0, turned[0])
+            regroup_v(1, turned[1])
+            turned = [turn(v_sb[:, head, :]) for head in range(2, 4)]
             quantise_v(0)
-            nc.vector.tensor_reduce(out=neg_max[:], in_=spread_t[:], axis=AX.X, op=ALU.max)
+            nc.vector.tensor_reduce(out=minus_g[:], in_=spread_t[:], axis=AX.X, op=ALU.max)
+            quantise_v(1)
+            regroup_v(2, turned[0])
+            regroup_v(3, turned[1])
 
         work = ctx.enter_context(tc.tile_pool(name="work", bufs=3))
         stats = ctx.enter_context(tc.tile_pool(name="stats", bufs=4))
-        attn_banks = ctx.enter_context(tc.psum_pool(name="attn_banks", bufs=3))
-        out_banks = ctx.enter_context(tc.psum_pool(name="out_banks", bufs=2))
+        u_banks = ctx.enter_context(tc.psum_pool(name="u_banks", bufs=3))
+        attn_banks = ctx.enter_context(tc.psum_pool(name="attn_banks", bufs=1))
+        out_banks = ctx.enter_context(tc.psum_pool(name="out_banks", bufs=1))
         live = {}
 
-        def row(b):
-            return neg[:, b // HEADS, b % HEADS, :]
-
-        def blend(b):
+        def finish_add(qt):
             nc.vector.scalar_tensor_tensor(
-                out=row(b), in0=row(b), scalar=neg_max[:, 0:1], in1=m[:, b // HEADS, :],
-                op0=ALU.subtract, op1=ALU.mult,
+                out=add_of(qt), in0=m_of(qt), scalar=minus_g[:, 0:1], in1=add_of(qt), op0=ALU.mult, op1=ALU.add
             )
 
+        def assemble(b):
+            qt, head = b // HEADS, b % HEADS
+            for half in range(HALVES):
+                bank = u_banks.tile([P, BANK], F32, name="u%d" % half)
+                live["u", b, half] = bank
+                for c in range(BANK // P):
+                    cols = slice(c * P, (c + 1) * P)
+                    chunk = half * (BANK // P) + c
+                    nc.tensor.matmul(
+                        out=bank[:, cols], lhsT=scores[:, qt // Q_HALF, head, qt % Q_HALF, chunk, :],
+                        rhs=ident_f32[:], is_transpose=True, start=True, stop=False,
+                    )
+                    nc.tensor.matmul(
+                        out=bank[:, cols], lhsT=add_t[:, qt, chunk, :],
+                        rhs=ident_f32[:], is_transpose=True, start=False, stop=True,
+                    )
+
         def row_max(b):
+            live["top", b] = stats.tile([P, HALVES], F32, name="top")
+            for half in range(HALVES):
+                nc.vector.tensor_reduce(
+                    out=live["top", b][:, half : half + 1], in_=live["u", b, half][:], axis=AX.X, op=ALU.max
+                )
+
+        def bias(b):
             live["bias", b] = stats.tile([P, 1], F32, name="bias")
-            nc.vector.tensor_reduce(out=live["bias", b][:], in_=row(b), axis=AX.X, op=ALU.min)
+            nc.vector.tensor_scalar(
+                out=live["bias", b][:], in0=live["top", b][:, 0:1], scalar1=live["top", b][:, 1:2], scalar2=-1.0,
+                op0=ALU.max, op1=ALU.mult,
+            )
 
         def exponential(b):
-            nc.scalar.activation(out=row(b), in_=row(b), func=ACT.Exp, bias=live["bias", b][:, 0:1], scale=-1.0)
+            live["sums", b] = stats.tile([P, HALVES], F32, name="sums")
+            for half in range(HALVES):
+                nc.scalar.activation(
+                    out=block(b)[:, half * BANK : (half + 1) * BANK], in_=live["u", b, half][:], func=ACT.Exp,
+                    bias=live["bias", b][:, 0:1], scale=1.0, accum_out=live["sums", b][:, half : half + 1],
+                )
 
-        def weigh(b):
+        def total(b):
             live["sum", b] = stats.tile([P, 1], F32, name="sum")
-            nc.vector.scalar_tensor_tensor(
-                out=row(b), in0=row(b), scalar=1.0, in1=m[:, b // HEADS, :],
-                op0=ALU.mult, op1=ALU.mult, accum_out=live["sum", b][:],
+            nc.vector.tensor_tensor(
+                out=live["sum", b][:], in0=live["sums", b][:, 0:1], in1=live["sums", b][:, 1:2], op=ALU.add
             )
 
         def reciprocal(b):
@@ -191,7 +274,12 @@ def tile_mhattention_own_kernel(tc, q, k, v, attn_mask, out):
 
         def normalise(b):
             live["attn", b] = work.tile([P, SEQ], BF16, name="attn")
-            nc.scalar.activation(out=live["attn", b][:], in_=row(b), func=ACT.Copy, scale=live["inv", b][:, 0:1])
+            if b % 4 == 1:
+                nc.vector.tensor_scalar(
+                    out=live["attn", b][:], in0=block(b), scalar1=live["inv", b][:, 0:1], scalar2=None, op0=ALU.mult
+                )
+            else:
+                nc.scalar.activation(out=live["attn", b][:], in_=block(b), func=ACT.Copy, scale=live["inv", b][:, 0:1])
 
         def transpose(b):
             live["attn_t", b] = attn_banks.tile([P, SEQ], BF16, name="attn_t")
@@ -233,27 +321,36 @@ def tile_mhattention_own_kernel(tc, q, k, v, attn_mask, out):
         def store(b):
             if b % HEADS == HEADS - 1:
                 qt = b // HEADS
-                out_sb = work.tile([P, HEADS * P], F32)
+                out_sb = work.tile([P, HEADS * P], F32, name="out_sb")
                 nc.scalar.copy(out=out_sb[:], in_=live["out", qt][:])
                 nc.sync.dma_start(
                     out=out_dram[:, :, qt * P : (qt + 1) * P], in_=out_sb[:].rearrange("p (n i) -> p n i", n=HEADS)
                 )
 
-        def stage(i, lag, work_on, *args):
-            if 0 <= i - lag < ROW_BLOCKS:
-                work_on(i - lag, *args)
+        def stage(b, work_on, *args):
+            if 0 <= b < ROW_BLOCKS:
+                work_on(b, *args)
 
-        for i in range(ROW_BLOCKS + LAG_STORE + 1):
-            stage(i, 0, blend)
-            stage(i, LAG_WEIGH, weigh)
-            stage(i, 0, row_max)
-            stage(i, LAG_WEIGH, reciprocal)
-            if i + 1 < HEADS:
-                quantise_v(i + 1)
-            stage(i, LAG_EXP, exponential)
-            stage(i, LAG_NORMALISE, normalise)
-            stage(i, LAG_NORMALISE, transpose)
-            stage(i, LAG_REGROUP, regroup, nc.scalar.copy if i < ROW_BLOCKS else nc.vector.tensor_copy)
-            stage(i, LAG_QUANTISE, quantise)
-            stage(i, LAG_QUANTISE, multiply)
-            stage(i, LAG_STORE, store)
+        finish_add(0)
+        weigh_vector(GPSIMD_BLOCKS)
+        assemble(0)
+        assemble(1)
+        for i in range(ROW_BLOCKS + 6):
+            stage(i - 5, multiply)
+            stage(i, row_max)
+            stage(i - 2, total)
+            stage(i, bias)
+            stage(i - 2, reciprocal)
+            stage(i - 1, exponential)
+            if i % HEADS == 1 and i // HEADS + 1 < Q_TILES:
+                finish_add(i // HEADS + 1)
+            if i % 2 == 0 and GPSIMD_BLOCKS + 1 + i // 2 < ROW_BLOCKS:
+                weigh_vector(GPSIMD_BLOCKS + 1 + i // 2)
+            stage(i + 2, assemble)
+            stage(i - 3, regroup, nc.scalar.copy if i < ROW_BLOCKS else nc.vector.tensor_copy)
+            stage(i - 2, normalise)
+            stage(i - 2, transpose)
+            if i < 2:
+                quantise_v(i + 2)
+            stage(i - 4, quantise)
+            stage(i - 5, store)

@@ -129,6 +129,13 @@ def tile_mhattention_own_kernel(tc, q, k, v, attn_mask, out):
                     )
                 return bank
 
+            def turn_words(source):
+                bank = turned_banks.tile([P, BANK], F32, name="turned")
+                for c in range(BANK // P):
+                    cols = slice(c * P, (c + 1) * P)
+                    nc.tensor.transpose(out=bank[:, cols], in_=source.bitcast(F32)[:, cols], identity=ident_f32[:])
+                return bank
+
             def make_m(qt):
                 bank = turn(mask_sb[qt][:])
                 nc.scalar.activation(out=m_of(qt), in_=bank[:], func=ACT.Copy, scale=1.0e-4, bias=1.0)
@@ -136,7 +143,7 @@ def tile_mhattention_own_kernel(tc, q, k, v, attn_mask, out):
             def make_ln(qt):
                 nc.scalar.activation(out=add_of(qt), in_=m_of(qt), func=ACT.Ln)
 
-            side_work = [(make_m, qt) for qt in range(Q_TILES)] + [(make_ln, qt) for qt in range(Q_TILES)]
+            side_work = [(make_m, qt) for qt in range(Q_TILES)] + [(make_ln, qt) for qt in range(5)]
             made_m, heads_done, to_weigh = [], [], [(t, head) for head in range(HEADS) for t in range(Q_HALF)]
             n_mins = 0
             pending = None
@@ -191,11 +198,11 @@ def tile_mhattention_own_kernel(tc, q, k, v, attn_mask, out):
             def regroup_v(head, bank):
                 v_grouped[head] = v_pool.tile([P, PASSES * P * PACK], BF16, name="v_grouped", align_bytes=64)
                 nc.scalar.copy(
-                    out=v_grouped[head][:].rearrange("p (ps d t) -> p ps d t", ps=PASSES, t=PACK),
-                    in_=bank[:].rearrange("p (ps t d) -> p ps d t", ps=PASSES, t=PACK),
+                    out=v_grouped[head][:].bitcast(F32).rearrange("p (ps d u) -> p ps d u", ps=PASSES, u=PACK // 2),
+                    in_=bank[:].rearrange("p (ps u d) -> p ps d u", ps=PASSES, u=PACK // 2),
                 )
 
-            turned = [turn(v_sb[:, head, :]) for head in range(2)]
+            turned = [turn_words(v_sb[:, head, :]) for head in range(2)]
             nc.vector.tensor_scalar(
                 out=spread[:], in0=last_min[:, 0:1].to_broadcast([P, P]),
                 scalar1=earlier_min[:, 0:1], scalar2=-1.0, op0=ALU.min, op1=ALU.mult,
@@ -204,12 +211,18 @@ def tile_mhattention_own_kernel(tc, q, k, v, attn_mask, out):
             nc.tensor.transpose(out=spread_t[:], in_=spread[:], identity=ident_f32[:])
             regroup_v(0, turned[0])
             regroup_v(1, turned[1])
-            turned = [turn(v_sb[:, head, :]) for head in range(2, 4)]
+            turned = [turn_words(v_sb[:, head, :]) for head in range(2, 4)]
+            for c in range(4):
+                bank = score_banks.tile([P, BANK], F32, name="bank")
+                nc.tensor.matmul(
+                    out=bank[:], lhsT=k_sb[:, 0, c * P : (c + 1) * P], rhs=q_sb[:, 0, 0:BANK], start=True, stop=True
+                )
             quantise_v(0)
             nc.vector.tensor_reduce(out=minus_g[:], in_=spread_t[:], axis=AX.X, op=ALU.max)
-            quantise_v(1)
             regroup_v(2, turned[0])
             regroup_v(3, turned[1])
+            for qt in range(5, Q_TILES):
+                make_ln(qt)
 
         work = ctx.enter_context(tc.tile_pool(name="work", bufs=3))
         stats = ctx.enter_context(tc.tile_pool(name="stats", bufs=4))
@@ -218,9 +231,10 @@ def tile_mhattention_own_kernel(tc, q, k, v, attn_mask, out):
         out_banks = ctx.enter_context(tc.psum_pool(name="out_banks", bufs=1))
         live = {}
 
-        def finish_add(qt):
+        def finish_add(qt, cols=slice(0, SEQ)):
             nc.vector.scalar_tensor_tensor(
-                out=add_of(qt), in0=m_of(qt), scalar=minus_g[:, 0:1], in1=add_of(qt), op0=ALU.mult, op1=ALU.add
+                out=add_of(qt)[:, cols], in0=m_of(qt)[:, cols], scalar=minus_g[:, 0:1], in1=add_of(qt)[:, cols],
+                op0=ALU.mult, op1=ALU.add,
             )
 
         def assemble(b):
@@ -274,26 +288,33 @@ def tile_mhattention_own_kernel(tc, q, k, v, attn_mask, out):
 
         def normalise(b):
             live["attn", b] = work.tile([P, SEQ], BF16, name="attn")
-            if b % 4 == 1:
+            if b % 4 == 1 or b >= ROW_BLOCKS - 2:
                 nc.vector.tensor_scalar(
                     out=live["attn", b][:], in0=block(b), scalar1=live["inv", b][:, 0:1], scalar2=None, op0=ALU.mult
                 )
             else:
                 nc.scalar.activation(out=live["attn", b][:], in_=block(b), func=ACT.Copy, scale=live["inv", b][:, 0:1])
 
+        def keep_clock(bank):
+            nc.tensor.matmul_mx(
+                out=bank[:], lhsT=v_codes[:, 0:P].bitcast(FP8X4), lhsT_scale=v_scales[:, 0:P],
+                rhs=v_codes[:, 0:BANK].bitcast(FP8X4), rhs_scale=v_scales[:, 0:BANK], start=True, stop=True,
+            )
+
         def transpose(b):
-            live["attn_t", b] = attn_banks.tile([P, SEQ], BF16, name="attn_t")
-            for c in range(CHUNKS):
+            live["attn_t", b] = attn_banks.tile([P, BANK], F32, name="attn_t")
+            keep_clock(live["attn_t", b])
+            for c in range(BANK // P):
+                cols = slice(c * P, (c + 1) * P)
                 nc.tensor.transpose(
-                    out=live["attn_t", b][:, c * P : (c + 1) * P], in_=live["attn", b][:, c * P : (c + 1) * P],
-                    identity=ident_bf16[:],
+                    out=live["attn_t", b][:, cols], in_=live["attn", b][:].bitcast(F32)[:, cols], identity=ident_f32[:]
                 )
 
         def regroup(b, copy):
             live["grouped", b] = work.tile([P, SEQ], BF16, name="grouped", align_bytes=64)
             copy(
-                out=live["grouped", b][:].rearrange("p (ps i t) -> p ps i t", ps=PASSES, t=PACK),
-                in_=live["attn_t", b][:].rearrange("p (ps t i) -> p ps i t", ps=PASSES, t=PACK),
+                out=live["grouped", b][:].bitcast(F32).rearrange("p (ps i u) -> p ps i u", ps=PASSES, u=PACK // 2),
+                in_=live["attn_t", b][:].rearrange("p (ps u i) -> p ps i u", ps=PASSES, u=PACK // 2),
             )
 
         def quantise(b):
@@ -331,10 +352,16 @@ def tile_mhattention_own_kernel(tc, q, k, v, attn_mask, out):
             if 0 <= b < ROW_BLOCKS:
                 work_on(b, *args)
 
-        finish_add(0)
+        for half in range(HALVES):
+            finish_add(0, slice(half * BANK, (half + 1) * BANK))
+        quantise_v(1)
         weigh_vector(GPSIMD_BLOCKS)
         assemble(0)
+        bank = attn_banks.tile([P, BANK], F32, name="attn_t")
+        keep_clock(bank)
+        keep_clock(bank)
         assemble(1)
+        keep_clock(bank)
         for i in range(ROW_BLOCKS + 6):
             stage(i - 5, multiply)
             stage(i, row_max)

@@ -16,18 +16,17 @@ P = 128
 HEADS = 4
 SEQ = 1024
 Q_TILES = SEQ // P
-ROW_BLOCKS = Q_TILES * HEADS
 CHUNKS = SEQ // P
 BANK = 512
 HALVES = SEQ // BANK
-Q_HALF = BANK // P
 PACK = 4
 PASSES = SEQ // (P * PACK)
 WORDS = PASSES * P
 SCALE = P ** -0.5
 FLOPS = 2 * 2 * HEADS * SEQ * SEQ * P
 
-GPSIMD_BLOCKS = 16
+T_TILES = Q_TILES // 2
+PAIRS = T_TILES * HEADS
 
 
 def tile_mhattention_own_kernel(tc, q, k, v, attn_mask, out):
@@ -42,9 +41,11 @@ def tile_mhattention_own_kernel(tc, q, k, v, attn_mask, out):
         ctx.enter_context(tc.manual_schedule())
         keep = ctx.enter_context(tc.tile_pool(name="keep", bufs=1))
 
-        scores = keep.tile([P, HALVES, HEADS, Q_HALF, CHUNKS, P], F32)
-        m_t = keep.tile([P, Q_TILES, CHUNKS, P], F32)
-        add_t = keep.tile([P, Q_TILES, CHUNKS, P], F32)
+        s_t = keep.tile([P, HEADS, T_TILES, CHUNKS, P], F32)
+        s_n = keep.tile([P, T_TILES, HEADS, SEQ], F32)
+        m_t = keep.tile([P, T_TILES, CHUNKS, P], F32)
+        m_n = keep.tile([P, T_TILES, SEQ], F32)
+        add_t = keep.tile([P, T_TILES, CHUNKS, P], F32)
         v_codes = keep.tile([P, HEADS * WORDS], U32, align_bytes=64)
         v_scales = keep.tile([P, HEADS * WORDS], U8, align_bytes=64)
         ident_bf16 = keep.tile([P, P], BF16)
@@ -58,9 +59,11 @@ def tile_mhattention_own_kernel(tc, q, k, v, attn_mask, out):
         make_identity(nc, ident_bf16[:])
         make_identity(nc, ident_f32[:])
 
-        def block(b):
-            qt, head = b // HEADS, b % HEADS
-            return scores[:, qt // Q_HALF, head, qt % Q_HALF].rearrange("p c i -> p (c i)")
+        def block_t(j):
+            return s_t[:, j % HEADS, j // HEADS].rearrange("p c i -> p (c i)")
+
+        def block_n(j):
+            return s_n[:, j // HEADS, j % HEADS, :]
 
         def m_of(qt):
             return m_t[:, qt].rearrange("p c i -> p (c i)")
@@ -68,11 +71,8 @@ def tile_mhattention_own_kernel(tc, q, k, v, attn_mask, out):
         def add_of(qt):
             return add_t[:, qt].rearrange("p c i -> p (c i)")
 
-        def weigh_gpsimd(b):
-            nc.gpsimd.tensor_tensor(out=block(b), in0=block(b), in1=m_of(b // HEADS), op=ALU.mult)
-
-        def weigh_vector(b):
-            nc.vector.tensor_tensor(out=block(b), in0=block(b), in1=m_of(b // HEADS), op=ALU.mult)
+        def weigh_scores(j):
+            nc.gpsimd.tensor_tensor(out=block_t(j), in0=block_t(j), in1=m_of(j // HEADS), op=ALU.mult)
 
         def quantise_v(head):
             words = slice(head * WORDS, (head + 1) * WORDS)
@@ -83,21 +83,22 @@ def tile_mhattention_own_kernel(tc, q, k, v, attn_mask, out):
             )
 
         v_grouped = {}
-        v_pool = ctx.enter_context(tc.tile_pool(name="v_pool", bufs=2))
+        v_pool = ctx.enter_context(tc.tile_pool(name="v_pool", bufs=HEADS))
 
         with ExitStack() as part1:
             loaded = part1.enter_context(tc.tile_pool(name="loaded", bufs=1))
-            mask_pool = part1.enter_context(tc.tile_pool(name="masks", bufs=4))
+            mask_pool = part1.enter_context(tc.tile_pool(name="masks", bufs=Q_TILES))
             score_banks = part1.enter_context(tc.psum_pool(name="score_banks", bufs=5))
             turned_banks = part1.enter_context(tc.psum_pool(name="turned_banks", bufs=2))
             max_bank = part1.enter_context(tc.psum_pool(name="max_bank", bufs=1))
             q_sb = loaded.tile([P, HEADS, SEQ], BF16)
             k_sb = loaded.tile([P, HEADS, SEQ], BF16)
             v_sb = loaded.tile([P, HEADS, SEQ], BF16)
-            PAIRS = HALVES * HEADS * CHUNKS // 2
-            mins = loaded.tile([P, PAIRS + PAIRS // 2], F32)
-            earlier_min = loaded.tile([P, 1], F32)
-            last_min = loaded.tile([P, 1], F32)
+            t_min = loaded.tile([P, PAIRS + PAIRS // 4], F32)
+            n_max = loaded.tile([P, PAIRS + PAIRS // 4], F32)
+            t_top = loaded.tile([P, 1], F32)
+            earlier_max = loaded.tile([P, 1], F32)
+            last_max = loaded.tile([P, 1], F32)
             spread = loaded.tile([P, P], F32)
             mask_sb = {}
 
@@ -143,57 +144,93 @@ def tile_mhattention_own_kernel(tc, q, k, v, attn_mask, out):
             def make_ln(qt):
                 nc.scalar.activation(out=add_of(qt), in_=m_of(qt), func=ACT.Ln)
 
-            side_work = [(make_m, qt) for qt in range(Q_TILES)] + [(make_ln, qt) for qt in range(5)]
-            made_m, heads_done, to_weigh = [], [], [(t, head) for head in range(HEADS) for t in range(Q_HALF)]
-            n_mins = 0
+            def make_m_plain(qt):
+                nc.gpsimd.tensor_scalar(
+                    out=m_n[:, qt, :], in0=mask_sb[T_TILES + qt][:], scalar1=1.0e-4, scalar2=1.0,
+                    op0=ALU.mult, op1=ALU.add,
+                )
+
+            def score_bank(lhs, rhs):
+                bank = score_banks.tile([P, BANK], F32, name="bank")
+                nc.tensor.matmul(out=bank[:], lhsT=lhs, rhs=rhs, start=True, stop=True)
+                return bank
+
+            def settle(stat, column, op):
+                nc.vector.tensor_reduce(out=stat[:, column : column + 1], in_=pending, axis=AX.XY, op=op)
+
+            side_work = [(make_m, qt) for qt in range(T_TILES)]
+            made_m, heads_done = [], []
+            to_weigh = [(t, head) for head in range(HEADS) for t in range(T_TILES)]
+            columns = 0
             pending = None
-            pair = 0
-            for half in range(HALVES):
-                queries = slice(half * BANK, (half + 1) * BANK)
-                for head in range(HEADS):
-                    for pr in range(CHUNKS // 2):
-                        last = pair == PAIRS - 1
-                        for c in (2 * pr, 2 * pr + 1):
-                            bank = score_banks.tile([P, BANK], F32, name="bank")
-                            nc.tensor.matmul(
-                                out=bank[:], lhsT=k_sb[:, head, c * P : (c + 1) * P], rhs=q_sb[:, head, queries],
-                                start=True, stop=True,
-                            )
-                            place = scores[:, half, head, :, c, :]
-                            bank_view = bank[:].rearrange("p (t i) -> p t i", t=Q_HALF)
-                            if pr % 2 == 0:
-                                nc.scalar.activation(out=place, in_=bank_view, func=ACT.Copy, scale=SCALE)
-                            else:
-                                if last and c == 2 * pr + 1:
-                                    nc.vector.tensor_reduce(
-                                        out=mins[:, n_mins : n_mins + 1], in_=pending, axis=AX.XY, op=ALU.min
-                                    )
-                                    n_mins += 1
-                                    column = last_min[:]
-                                else:
-                                    column = mins[:, n_mins : n_mins + 1]
-                                    n_mins += 1
-                                nc.vector.tensor_scalar(
-                                    out=place, in0=bank_view, scalar1=SCALE, scalar2=None,
-                                    op0=ALU.mult, op1=ALU.min, accum_out=column,
-                                )
-                        if pr % 2 == 0:
-                            pending = scores[:, half, head, :, 2 * pr : 2 * pr + 2, :].rearrange("p t c i -> p t (c i)")
-                            if side_work:
-                                work_on, qt = side_work.pop(0)
-                                work_on(qt)
-                                if work_on == make_m:
-                                    made_m.append(qt)
-                        elif not last:
-                            nc.vector.tensor_reduce(out=mins[:, n_mins : n_mins + 1], in_=pending, axis=AX.XY, op=ALU.min)
-                            n_mins += 1
-                        pair += 1
-                        if half == 0 and pr == CHUNKS // 2 - 1:
-                            heads_done.append(head)
-                        while to_weigh and to_weigh[0][0] in made_m and to_weigh[0][1] in heads_done:
-                            t, done_head = to_weigh.pop(0)
-                            weigh_gpsimd(t * HEADS + done_head)
-            nc.vector.tensor_reduce(out=earlier_min[:], in_=mins[:, 0:n_mins], axis=AX.X, op=ALU.min)
+            for pair in range(PAIRS):
+                head, pr = pair // (CHUNKS // 2), pair % (CHUNKS // 2)
+                fused = pair % 4 == 3
+                for c in (2 * pr, 2 * pr + 1):
+                    bank = score_bank(k_sb[:, head, c * P : (c + 1) * P], q_sb[:, head, 0:BANK])
+                    place = s_t[:, head, :, c, :]
+                    bank_view = bank[:].rearrange("p (t i) -> p t i", t=T_TILES)
+                    if fused:
+                        nc.vector.tensor_scalar(
+                            out=place, in0=bank_view, scalar1=SCALE, scalar2=None,
+                            op0=ALU.mult, op1=ALU.min, accum_out=t_min[:, columns : columns + 1],
+                        )
+                        columns += 1
+                    else:
+                        nc.scalar.activation(out=place, in_=bank_view, func=ACT.Copy, scale=SCALE)
+                if pending is not None:
+                    settle(t_min, columns, ALU.min)
+                    columns += 1
+                    pending = None
+                if not fused:
+                    pending = s_t[:, head, :, 2 * pr : 2 * pr + 2, :].rearrange("p t c i -> p t (c i)")
+                    if side_work:
+                        work_on, qt = side_work.pop(0)
+                        work_on(qt)
+                        made_m.append(qt)
+                if pr == CHUNKS // 2 - 1:
+                    heads_done.append(head)
+                while to_weigh and to_weigh[0][0] in made_m and to_weigh[0][1] in heads_done:
+                    t, done_head = to_weigh.pop(0)
+                    weigh_scores(t * HEADS + done_head)
+                    if t == T_TILES - 1:
+                        make_m_plain(done_head)
+            nc.vector.tensor_reduce(out=t_top[:], in_=t_min[:, 0:columns], axis=AX.X, op=ALU.min)
+            side_work = [(make_ln, qt) for qt in range(T_TILES)]
+            columns = 0
+            for pair in range(PAIRS):
+                t, head = pair // HEADS, pair % HEADS
+                fused = pair % 4 == 3
+                queries = slice((T_TILES + t) * P, (T_TILES + t + 1) * P)
+                for half in range(HALVES):
+                    keys = slice(half * BANK, (half + 1) * BANK)
+                    bank = score_bank(q_sb[:, head, queries], k_sb[:, head, keys])
+                    place = s_n[:, t, head, keys]
+                    if fused:
+                        last = pair == PAIRS - 1 and half == HALVES - 1
+                        if last:
+                            settle(n_max, columns, ALU.max)
+                            columns += 1
+                            pending = None
+                        nc.vector.tensor_scalar(
+                            out=place, in0=bank[:], scalar1=-SCALE, scalar2=None, op0=ALU.mult, op1=ALU.max,
+                            accum_out=last_max[:] if last else n_max[:, columns : columns + 1],
+                        )
+                        columns += 0 if last else 1
+                    else:
+                        nc.scalar.activation(out=place, in_=bank[:], func=ACT.Copy, scale=-SCALE)
+                if pending is not None:
+                    settle(n_max, columns, ALU.max)
+                    columns += 1
+                    pending = None
+                if not fused:
+                    pending = s_n[:, t, head, :].rearrange("p (c i) -> p c i", i=P)
+                    if side_work and pair >= 4:
+                        work_on, qt = side_work.pop(0)
+                        work_on(qt)
+                if pair == 0:
+                    nc.vector.tensor_scalar(out=t_top[:], in0=t_top[:], scalar1=-1.0, scalar2=None, op0=ALU.mult)
+            nc.vector.tensor_reduce(out=earlier_max[:], in_=n_max[:, 0:columns], axis=AX.X, op=ALU.max)
 
             def regroup_v(head, bank):
                 v_grouped[head] = v_pool.tile([P, PASSES * P * PACK], BF16, name="v_grouped", align_bytes=64)
@@ -204,32 +241,26 @@ def tile_mhattention_own_kernel(tc, q, k, v, attn_mask, out):
 
             turned = [turn_words(v_sb[:, head, :]) for head in range(2)]
             nc.vector.tensor_scalar(
-                out=spread[:], in0=last_min[:, 0:1].to_broadcast([P, P]),
-                scalar1=earlier_min[:, 0:1], scalar2=-1.0, op0=ALU.min, op1=ALU.mult,
+                out=spread[:], in0=last_max[:, 0:1].to_broadcast([P, P]),
+                scalar1=earlier_max[:, 0:1], scalar2=t_top[:, 0:1], op0=ALU.max, op1=ALU.max,
             )
             spread_t = max_bank.tile([P, P], F32)
             nc.tensor.transpose(out=spread_t[:], in_=spread[:], identity=ident_f32[:])
             regroup_v(0, turned[0])
             regroup_v(1, turned[1])
             turned = [turn_words(v_sb[:, head, :]) for head in range(2, 4)]
-            for c in range(4):
-                bank = score_banks.tile([P, BANK], F32, name="bank")
-                nc.tensor.matmul(
-                    out=bank[:], lhsT=k_sb[:, 0, c * P : (c + 1) * P], rhs=q_sb[:, 0, 0:BANK], start=True, stop=True
-                )
             quantise_v(0)
             nc.vector.tensor_reduce(out=minus_g[:], in_=spread_t[:], axis=AX.X, op=ALU.max)
             regroup_v(2, turned[0])
             regroup_v(3, turned[1])
-            for qt in range(5, Q_TILES):
-                make_ln(qt)
 
         work = ctx.enter_context(tc.tile_pool(name="work", bufs=3))
         stats = ctx.enter_context(tc.tile_pool(name="stats", bufs=4))
-        u_banks = ctx.enter_context(tc.psum_pool(name="u_banks", bufs=3))
-        attn_banks = ctx.enter_context(tc.psum_pool(name="attn_banks", bufs=1))
+        u_banks = ctx.enter_context(tc.psum_pool(name="u_banks", bufs=2))
+        attn_banks = ctx.enter_context(tc.psum_pool(name="attn_banks", bufs=2))
         out_banks = ctx.enter_context(tc.psum_pool(name="out_banks", bufs=1))
         live = {}
+        T, N = "t", "n"
 
         def finish_add(qt, cols=slice(0, SEQ)):
             nc.vector.scalar_tensor_tensor(
@@ -237,147 +268,179 @@ def tile_mhattention_own_kernel(tc, q, k, v, attn_mask, out):
                 op0=ALU.mult, op1=ALU.add,
             )
 
-        def assemble(b):
-            qt, head = b // HEADS, b % HEADS
+        def assemble(j):
+            qt, head = j // HEADS, j % HEADS
             for half in range(HALVES):
                 bank = u_banks.tile([P, BANK], F32, name="u%d" % half)
-                live["u", b, half] = bank
+                live["u", j, half] = bank
                 for c in range(BANK // P):
                     cols = slice(c * P, (c + 1) * P)
                     chunk = half * (BANK // P) + c
                     nc.tensor.matmul(
-                        out=bank[:, cols], lhsT=scores[:, qt // Q_HALF, head, qt % Q_HALF, chunk, :],
-                        rhs=ident_f32[:], is_transpose=True, start=True, stop=False,
+                        out=bank[:, cols], lhsT=s_t[:, head, qt, chunk, :], rhs=ident_f32[:],
+                        is_transpose=True, start=True, stop=False,
                     )
                     nc.tensor.matmul(
-                        out=bank[:, cols], lhsT=add_t[:, qt, chunk, :],
-                        rhs=ident_f32[:], is_transpose=True, start=False, stop=True,
+                        out=bank[:, cols], lhsT=add_t[:, qt, chunk, :], rhs=ident_f32[:],
+                        is_transpose=True, start=False, stop=True,
                     )
 
-        def row_max(b):
-            live["top", b] = stats.tile([P, HALVES], F32, name="top")
+        def row_max_t(j):
+            live["top", j] = stats.tile([P, HALVES], F32, name="top")
             for half in range(HALVES):
                 nc.vector.tensor_reduce(
-                    out=live["top", b][:, half : half + 1], in_=live["u", b, half][:], axis=AX.X, op=ALU.max
+                    out=live["top", j][:, half : half + 1], in_=live["u", j, half][:], axis=AX.X, op=ALU.max
                 )
 
-        def bias(b):
-            live["bias", b] = stats.tile([P, 1], F32, name="bias")
+        def bias_t(j):
+            live["bias", T, j] = stats.tile([P, 1], F32, name="bias_t")
             nc.vector.tensor_scalar(
-                out=live["bias", b][:], in0=live["top", b][:, 0:1], scalar1=live["top", b][:, 1:2], scalar2=-1.0,
+                out=live["bias", T, j][:], in0=live["top", j][:, 0:1], scalar1=live["top", j][:, 1:2], scalar2=-1.0,
                 op0=ALU.max, op1=ALU.mult,
             )
 
-        def exponential(b):
-            live["sums", b] = stats.tile([P, HALVES], F32, name="sums")
+        def exponential_t(j):
+            live["sums", j] = stats.tile([P, HALVES], F32, name="sums")
             for half in range(HALVES):
                 nc.scalar.activation(
-                    out=block(b)[:, half * BANK : (half + 1) * BANK], in_=live["u", b, half][:], func=ACT.Exp,
-                    bias=live["bias", b][:, 0:1], scale=1.0, accum_out=live["sums", b][:, half : half + 1],
+                    out=block_t(j)[:, half * BANK : (half + 1) * BANK], in_=live["u", j, half][:], func=ACT.Exp,
+                    bias=live["bias", T, j][:, 0:1], scale=1.0, accum_out=live["sums", j][:, half : half + 1],
                 )
 
-        def total(b):
-            live["sum", b] = stats.tile([P, 1], F32, name="sum")
-            nc.vector.tensor_tensor(
-                out=live["sum", b][:], in0=live["sums", b][:, 0:1], in1=live["sums", b][:, 1:2], op=ALU.add
+        def total_t(j):
+            live["sum", T, j] = stats.tile([P, 1], F32, name="sum_t")
+            nc.vector.tensor_reduce(out=live["sum", T, j][:], in_=live["sums", j][:], axis=AX.X, op=ALU.add)
+
+        def blend(j):
+            nc.vector.scalar_tensor_tensor(
+                out=block_n(j), in0=block_n(j), scalar=minus_g[:, 0:1], in1=m_n[:, j // HEADS, :],
+                op0=ALU.subtract, op1=ALU.mult,
             )
 
-        def reciprocal(b):
-            live["inv", b] = stats.tile([P, 1], F32, name="inv")
-            nc.vector.reciprocal(out=live["inv", b][:], in_=live["sum", b][:])
+        def row_max_n(j):
+            live["bias", N, j] = stats.tile([P, 1], F32, name="bias_n")
+            nc.vector.tensor_reduce(out=live["bias", N, j][:], in_=block_n(j), axis=AX.X, op=ALU.min)
 
-        def normalise(b):
-            live["attn", b] = work.tile([P, SEQ], BF16, name="attn")
-            if b % 4 == 1 or b >= ROW_BLOCKS - 2:
-                nc.vector.tensor_scalar(
-                    out=live["attn", b][:], in0=block(b), scalar1=live["inv", b][:, 0:1], scalar2=None, op0=ALU.mult
+        def exponential_n(j):
+            nc.scalar.activation(
+                out=block_n(j), in_=block_n(j), func=ACT.Exp, bias=live["bias", N, j][:, 0:1], scale=-1.0
+            )
+
+        def weigh_n(j):
+            live["sum", N, j] = stats.tile([P, 1], F32, name="sum_n")
+            nc.vector.scalar_tensor_tensor(
+                out=block_n(j), in0=block_n(j), scalar=1.0, in1=m_n[:, j // HEADS, :],
+                op0=ALU.mult, op1=ALU.mult, accum_out=live["sum", N, j][:],
+            )
+
+        def reciprocal(j, kind):
+            live["inv", kind, j] = stats.tile([P, 1], F32, name="inv_" + kind)
+            nc.vector.reciprocal(out=live["inv", kind, j][:], in_=live["sum", kind, j][:])
+
+        def normalise(j, kind, engine):
+            live["attn", kind, j] = work.tile([P, SEQ], BF16, name="attn_" + kind)
+            rows = block_t(j) if kind == T else block_n(j)
+            if engine == "scalar":
+                nc.scalar.activation(
+                    out=live["attn", kind, j][:], in_=rows, func=ACT.Copy, scale=live["inv", kind, j][:, 0:1]
+                )
+            elif engine == "gpsimd":
+                nc.gpsimd.tensor_scalar(
+                    out=live["attn", kind, j][:], in0=rows, scalar1=live["inv", kind, j][:, 0:1], scalar2=0.0,
+                    op0=ALU.mult, op1=ALU.add,
                 )
             else:
-                nc.scalar.activation(out=live["attn", b][:], in_=block(b), func=ACT.Copy, scale=live["inv", b][:, 0:1])
+                nc.vector.tensor_scalar(
+                    out=live["attn", kind, j][:], in0=rows, scalar1=live["inv", kind, j][:, 0:1], scalar2=None,
+                    op0=ALU.mult,
+                )
 
-        def keep_clock(bank):
-            nc.tensor.matmul_mx(
-                out=bank[:], lhsT=v_codes[:, 0:P].bitcast(FP8X4), lhsT_scale=v_scales[:, 0:P],
-                rhs=v_codes[:, 0:BANK].bitcast(FP8X4), rhs_scale=v_scales[:, 0:BANK], start=True, stop=True,
-            )
-
-        def transpose(b):
-            live["attn_t", b] = attn_banks.tile([P, BANK], F32, name="attn_t")
-            keep_clock(live["attn_t", b])
+        def transpose(j, kind):
+            live["attn_t", kind, j] = attn_banks.tile([P, BANK], F32, name="attn_t")
             for c in range(BANK // P):
                 cols = slice(c * P, (c + 1) * P)
                 nc.tensor.transpose(
-                    out=live["attn_t", b][:, cols], in_=live["attn", b][:].bitcast(F32)[:, cols], identity=ident_f32[:]
+                    out=live["attn_t", kind, j][:, cols], in_=live["attn", kind, j][:].bitcast(F32)[:, cols],
+                    identity=ident_f32[:],
                 )
 
-        def regroup(b, copy):
-            live["grouped", b] = work.tile([P, SEQ], BF16, name="grouped", align_bytes=64)
+        def regroup(j, kind, copy):
+            live["grouped", kind, j] = work.tile([P, SEQ], BF16, name="grouped", align_bytes=64)
             copy(
-                out=live["grouped", b][:].bitcast(F32).rearrange("p (ps i u) -> p ps i u", ps=PASSES, u=PACK // 2),
-                in_=live["attn_t", b][:].rearrange("p (ps u i) -> p ps i u", ps=PASSES, u=PACK // 2),
+                out=live["grouped", kind, j][:].bitcast(F32).rearrange("p (ps i u) -> p ps i u", ps=PASSES, u=PACK // 2),
+                in_=live["attn_t", kind, j][:].rearrange("p (ps u i) -> p ps i u", ps=PASSES, u=PACK // 2),
             )
 
-        def quantise(b):
-            live["codes", b] = work.tile([P, WORDS], U32, name="codes", align_bytes=64)
-            live["scales", b] = work.tile([P, WORDS], U8, name="scales", align_bytes=64)
+        def quantise(j, kind):
+            live["codes", kind, j] = work.tile([P, WORDS], U32, name="codes", align_bytes=64)
+            live["scales", kind, j] = work.tile([P, WORDS], U8, name="scales", align_bytes=64)
             nc.vector.quantize_mx(
-                out=live["codes", b][:].bitcast(FP8X4), scales=live["scales", b][:], in_=live["grouped", b][:]
+                out=live["codes", kind, j][:].bitcast(FP8X4), scales=live["scales", kind, j][:],
+                in_=live["grouped", kind, j][:],
             )
 
-        def multiply(b):
-            head = b % HEADS
+        def multiply(j, kind):
+            head, qt = j % HEADS, j // HEADS
             if head == 0:
-                live["out", b // HEADS] = out_banks.tile([P, HEADS * P], F32, name="out_bank")
+                live["out", kind, qt] = out_banks.tile([P, HEADS * P], F32, name="out_" + kind)
             for ps in range(PASSES):
                 v_words = slice(head * WORDS + ps * P, head * WORDS + (ps + 1) * P)
                 attn_words = slice(ps * P, (ps + 1) * P)
                 nc.tensor.matmul_mx(
-                    out=live["out", b // HEADS][:, head * P : (head + 1) * P],
+                    out=live["out", kind, qt][:, head * P : (head + 1) * P],
                     lhsT=v_codes[:, v_words].bitcast(FP8X4), lhsT_scale=v_scales[:, v_words],
-                    rhs=live["codes", b][:, attn_words].bitcast(FP8X4),
-                    rhs_scale=live["scales", b][:, attn_words],
+                    rhs=live["codes", kind, j][:, attn_words].bitcast(FP8X4),
+                    rhs_scale=live["scales", kind, j][:, attn_words],
                     start=(ps == 0), stop=(ps == PASSES - 1),
                 )
 
-        def store(b):
-            if b % HEADS == HEADS - 1:
-                qt = b // HEADS
+        def store(j, kind):
+            if j % HEADS == HEADS - 1:
+                qt = j // HEADS
+                place = qt if kind == T else T_TILES + qt
                 out_sb = work.tile([P, HEADS * P], F32, name="out_sb")
-                nc.scalar.copy(out=out_sb[:], in_=live["out", qt][:])
+                nc.scalar.copy(out=out_sb[:], in_=live["out", kind, qt][:])
                 nc.sync.dma_start(
-                    out=out_dram[:, :, qt * P : (qt + 1) * P], in_=out_sb[:].rearrange("p (n i) -> p n i", n=HEADS)
+                    out=out_dram[:, :, place * P : (place + 1) * P],
+                    in_=out_sb[:].rearrange("p (n i) -> p n i", n=HEADS),
                 )
 
-        def stage(b, work_on, *args):
-            if 0 <= b < ROW_BLOCKS:
-                work_on(b, *args)
+        def stage(j, work_on, *args):
+            if 0 <= j < PAIRS:
+                work_on(j, *args)
 
+        blend(0)
         for half in range(HALVES):
             finish_add(0, slice(half * BANK, (half + 1) * BANK))
-        quantise_v(1)
-        weigh_vector(GPSIMD_BLOCKS)
+        row_max_n(0)
         assemble(0)
-        bank = attn_banks.tile([P, BANK], F32, name="attn_t")
-        keep_clock(bank)
-        keep_clock(bank)
-        assemble(1)
-        keep_clock(bank)
-        for i in range(ROW_BLOCKS + 6):
-            stage(i - 5, multiply)
-            stage(i, row_max)
-            stage(i - 2, total)
-            stage(i, bias)
-            stage(i - 2, reciprocal)
-            stage(i - 1, exponential)
-            if i % HEADS == 1 and i // HEADS + 1 < Q_TILES:
-                finish_add(i // HEADS + 1)
-            if i % 2 == 0 and GPSIMD_BLOCKS + 1 + i // 2 < ROW_BLOCKS:
-                weigh_vector(GPSIMD_BLOCKS + 1 + i // 2)
-            stage(i + 2, assemble)
-            stage(i - 3, regroup, nc.scalar.copy if i < ROW_BLOCKS else nc.vector.tensor_copy)
-            stage(i - 2, normalise)
-            stage(i - 2, transpose)
-            if i < 2:
-                quantise_v(i + 2)
-            stage(i - 4, quantise)
-            stage(i - 5, store)
+        exponential_n(0)
+        for j in range(PAIRS + 3):
+            copy = nc.scalar.copy if j < PAIRS else nc.vector.tensor_copy
+            stage(j - 1, transpose, T)
+            stage(j, row_max_t)
+            stage(j, weigh_n)
+            stage(j, bias_t)
+            stage(j, exponential_t)
+            stage(j + 1, blend)
+            stage(j, reciprocal, N)
+            stage(j, normalise, N, "scalar" if j < PAIRS - 1 else "vector")
+            stage(j + 1, assemble)
+            stage(j - 1, quantise, N)
+            stage(j - 1, multiply, N)
+            stage(j, transpose, N)
+            stage(j + 1, row_max_n)
+            stage(j, total_t)
+            stage(j - 1, regroup, T, copy)
+            stage(j + 1, exponential_n)
+            stage(j, regroup, N, copy)
+            if j % HEADS == 1 and j // HEADS + 1 < T_TILES:
+                finish_add(j // HEADS + 1)
+            if j < 3:
+                quantise_v(j + 1)
+            stage(j - 1, quantise, T)
+            stage(j, reciprocal, T)
+            stage(j, normalise, T, "gpsimd" if j < PAIRS - 1 else "vector")
+            stage(j - 1, multiply, T)
+            stage(j - 1, store, N)
+            stage(j - 1, store, T)

@@ -82,6 +82,7 @@ def tile_mhattention_own_kernel(tc, q, k, v, attn_mask, out):
                 in_=v_grouped[head][:],
             )
 
+        stats = ctx.enter_context(tc.tile_pool(name="stats", bufs=4))
         v_grouped = {}
         v_pool = ctx.enter_context(tc.tile_pool(name="v_pool", bufs=HEADS))
 
@@ -94,7 +95,7 @@ def tile_mhattention_own_kernel(tc, q, k, v, attn_mask, out):
             q_sb = loaded.tile([P, HEADS, SEQ], BF16)
             k_sb = loaded.tile([P, HEADS, SEQ], BF16)
             v_sb = loaded.tile([P, HEADS, SEQ], BF16)
-            t_min = loaded.tile([P, PAIRS + PAIRS // 4], F32)
+            t_min = loaded.tile([P, 2 * PAIRS], F32)
             n_max = loaded.tile([P, PAIRS + PAIRS // 4], F32)
             t_top = loaded.tile([P, 1], F32)
             earlier_max = loaded.tile([P, 1], F32)
@@ -165,7 +166,7 @@ def tile_mhattention_own_kernel(tc, q, k, v, attn_mask, out):
             pending = None
             for pair in range(PAIRS):
                 head, pr = pair // (CHUNKS // 2), pair % (CHUNKS // 2)
-                fused = pair % 4 == 3
+                fused = pr == 3 or (pr == 1 and head < 2)
                 for c in (2 * pr, 2 * pr + 1):
                     bank = score_bank(k_sb[:, head, c * P : (c + 1) * P], q_sb[:, head, 0:BANK])
                     place = s_t[:, head, :, c, :]
@@ -240,22 +241,21 @@ def tile_mhattention_own_kernel(tc, q, k, v, attn_mask, out):
                 )
 
             turned = [turn_words(v_sb[:, head, :]) for head in range(2)]
+            regroup_v(0, turned[0])
+            regroup_v(1, turned[1])
+            turned = [turn_words(v_sb[:, head, :]) for head in range(2, 4)]
             nc.vector.tensor_scalar(
                 out=spread[:], in0=last_max[:, 0:1].to_broadcast([P, P]),
                 scalar1=earlier_max[:, 0:1], scalar2=t_top[:, 0:1], op0=ALU.max, op1=ALU.max,
             )
             spread_t = max_bank.tile([P, P], F32)
             nc.tensor.transpose(out=spread_t[:], in_=spread[:], identity=ident_f32[:])
-            regroup_v(0, turned[0])
-            regroup_v(1, turned[1])
-            turned = [turn_words(v_sb[:, head, :]) for head in range(2, 4)]
             quantise_v(0)
             nc.vector.tensor_reduce(out=minus_g[:], in_=spread_t[:], axis=AX.X, op=ALU.max)
             regroup_v(2, turned[0])
             regroup_v(3, turned[1])
 
         work = ctx.enter_context(tc.tile_pool(name="work", bufs=3))
-        stats = ctx.enter_context(tc.tile_pool(name="stats", bufs=4))
         u_banks = ctx.enter_context(tc.psum_pool(name="u_banks", bufs=2))
         attn_banks = ctx.enter_context(tc.psum_pool(name="attn_banks", bufs=2))
         out_banks = ctx.enter_context(tc.psum_pool(name="out_banks", bufs=1))
@@ -337,17 +337,23 @@ def tile_mhattention_own_kernel(tc, q, k, v, attn_mask, out):
             live["inv", kind, j] = stats.tile([P, 1], F32, name="inv_" + kind)
             nc.vector.reciprocal(out=live["inv", kind, j][:], in_=live["sum", kind, j][:])
 
+        def normalise_t(j):
+            live["attn", T, j] = work.tile([P, SEQ], BF16, name="attn_t")
+            nc.gpsimd.tensor_scalar(
+                out=live["attn", T, j][:, 0:BANK], in0=block_t(j)[:, 0:BANK], scalar1=live["inv", T, j][:, 0:1],
+                scalar2=0.0, op0=ALU.mult, op1=ALU.add,
+            )
+            nc.scalar.activation(
+                out=live["attn", T, j][:, BANK:SEQ], in_=block_t(j)[:, BANK:SEQ], func=ACT.Copy,
+                scale=live["inv", T, j][:, 0:1],
+            )
+
         def normalise(j, kind, engine):
             live["attn", kind, j] = work.tile([P, SEQ], BF16, name="attn_" + kind)
             rows = block_t(j) if kind == T else block_n(j)
             if engine == "scalar":
                 nc.scalar.activation(
                     out=live["attn", kind, j][:], in_=rows, func=ACT.Copy, scale=live["inv", kind, j][:, 0:1]
-                )
-            elif engine == "gpsimd":
-                nc.gpsimd.tensor_scalar(
-                    out=live["attn", kind, j][:], in0=rows, scalar1=live["inv", kind, j][:, 0:1], scalar2=0.0,
-                    op0=ALU.mult, op1=ALU.add,
                 )
             else:
                 nc.vector.tensor_scalar(
@@ -417,6 +423,9 @@ def tile_mhattention_own_kernel(tc, q, k, v, attn_mask, out):
         exponential_n(0)
         for j in range(PAIRS + 3):
             copy = nc.scalar.copy if j < PAIRS else nc.vector.tensor_copy
+            if j < PAIRS:
+                stage(j - 1, normalise_t)
+            stage(j + 1, assemble)
             stage(j - 1, transpose, T)
             stage(j, row_max_t)
             stage(j, weigh_n)
@@ -425,8 +434,8 @@ def tile_mhattention_own_kernel(tc, q, k, v, attn_mask, out):
             stage(j + 1, blend)
             stage(j, reciprocal, N)
             stage(j, normalise, N, "scalar" if j < PAIRS - 1 else "vector")
-            stage(j + 1, assemble)
             stage(j - 1, quantise, N)
+            stage(j - 2, multiply, T)
             stage(j - 1, multiply, N)
             stage(j, transpose, N)
             stage(j + 1, row_max_n)
@@ -440,7 +449,7 @@ def tile_mhattention_own_kernel(tc, q, k, v, attn_mask, out):
                 quantise_v(j + 1)
             stage(j - 1, quantise, T)
             stage(j, reciprocal, T)
-            stage(j, normalise, T, "gpsimd" if j < PAIRS - 1 else "vector")
-            stage(j - 1, multiply, T)
+            if j == PAIRS - 1:
+                normalise(j, T, "vector")
             stage(j - 1, store, N)
-            stage(j - 1, store, T)
+            stage(j - 2, store, T)

@@ -26,6 +26,7 @@ SCALE = P ** -0.5
 FLOPS = 2 * 2 * HEADS * SEQ * SEQ * P
 
 T_TILES = Q_TILES // 2
+VECTOR_PRODUCTS = (11, 15)
 PAIRS = T_TILES * HEADS
 
 
@@ -71,8 +72,14 @@ def tile_mhattention_own_kernel(tc, q, k, v, attn_mask, out):
         def add_of(qt):
             return add_t[:, qt].rearrange("p c i -> p (c i)")
 
-        def weigh_scores(j):
-            nc.gpsimd.tensor_tensor(out=block_t(j), in0=block_t(j), in1=m_of(j // HEADS), op=ALU.mult)
+        def weigh_scores(engine, j, cols=slice(0, SEQ)):
+            rows = block_t(j)[:, cols]
+            engine.tensor_tensor(out=rows, in0=rows, in1=m_of(j // HEADS)[:, cols], op=ALU.mult)
+
+        def make_m_plain(qt):
+            nc.scalar.activation(
+                out=m_n[:, qt, :], in_=mask_sb[T_TILES + qt][:], func=ACT.Copy, scale=1.0e-4, bias=1.0
+            )
 
         def quantise_v(head):
             words = slice(head * WORDS, (head + 1) * WORDS)
@@ -84,11 +91,12 @@ def tile_mhattention_own_kernel(tc, q, k, v, attn_mask, out):
 
         stats = ctx.enter_context(tc.tile_pool(name="stats", bufs=4))
         v_grouped = {}
+        mask_sb = {}
+        mask_pool = ctx.enter_context(tc.tile_pool(name="masks", bufs=Q_TILES))
         v_pool = ctx.enter_context(tc.tile_pool(name="v_pool", bufs=HEADS))
 
         with ExitStack() as part1:
             loaded = part1.enter_context(tc.tile_pool(name="loaded", bufs=1))
-            mask_pool = part1.enter_context(tc.tile_pool(name="masks", bufs=Q_TILES))
             score_banks = part1.enter_context(tc.psum_pool(name="score_banks", bufs=5))
             turned_banks = part1.enter_context(tc.psum_pool(name="turned_banks", bufs=2))
             max_bank = part1.enter_context(tc.psum_pool(name="max_bank", bufs=1))
@@ -101,7 +109,6 @@ def tile_mhattention_own_kernel(tc, q, k, v, attn_mask, out):
             earlier_max = loaded.tile([P, 1], F32)
             last_max = loaded.tile([P, 1], F32)
             spread = loaded.tile([P, P], F32)
-            mask_sb = {}
 
             def load_mask(qt):
                 mask_sb[qt] = mask_pool.tile([P, SEQ], BF16, name="mask_sb")
@@ -145,12 +152,6 @@ def tile_mhattention_own_kernel(tc, q, k, v, attn_mask, out):
             def make_ln(qt):
                 nc.scalar.activation(out=add_of(qt), in_=m_of(qt), func=ACT.Ln)
 
-            def make_m_plain(qt):
-                nc.gpsimd.tensor_scalar(
-                    out=m_n[:, qt, :], in0=mask_sb[T_TILES + qt][:], scalar1=1.0e-4, scalar2=1.0,
-                    op0=ALU.mult, op1=ALU.add,
-                )
-
             def score_bank(lhs, rhs):
                 bank = score_banks.tile([P, BANK], F32, name="bank")
                 nc.tensor.matmul(out=bank[:], lhsT=lhs, rhs=rhs, start=True, stop=True)
@@ -160,8 +161,16 @@ def tile_mhattention_own_kernel(tc, q, k, v, attn_mask, out):
                 nc.vector.tensor_reduce(out=stat[:, column : column + 1], in_=pending, axis=AX.XY, op=op)
 
             side_work = [(make_m, qt) for qt in range(T_TILES)]
-            made_m, heads_done = [], []
-            to_weigh = [(t, head) for head in range(HEADS) for t in range(T_TILES)]
+            to_weigh = []
+            for head in range(HEADS):
+                pairs_of_head = [1, 3] if head == 0 else [3]
+                for i, pr in enumerate(pairs_of_head):
+                    width = SEQ // len(pairs_of_head)
+                    for t in range(T_TILES):
+                        j = t * HEADS + head
+                        if j not in VECTOR_PRODUCTS:
+                            to_weigh.append((head * (CHUNKS // 2) + pr, t, j, slice(i * width, (i + 1) * width)))
+            made_m = []
             columns = 0
             pending = None
             for pair in range(PAIRS):
@@ -189,15 +198,11 @@ def tile_mhattention_own_kernel(tc, q, k, v, attn_mask, out):
                         work_on, qt = side_work.pop(0)
                         work_on(qt)
                         made_m.append(qt)
-                if pr == CHUNKS // 2 - 1:
-                    heads_done.append(head)
-                while to_weigh and to_weigh[0][0] in made_m and to_weigh[0][1] in heads_done:
-                    t, done_head = to_weigh.pop(0)
-                    weigh_scores(t * HEADS + done_head)
-                    if t == T_TILES - 1:
-                        make_m_plain(done_head)
+                while to_weigh and to_weigh[0][0] <= pair and to_weigh[0][1] in made_m:
+                    after, t, j, cols = to_weigh.pop(0)
+                    weigh_scores(nc.gpsimd, j, cols)
             nc.vector.tensor_reduce(out=t_top[:], in_=t_min[:, 0:columns], axis=AX.X, op=ALU.min)
-            side_work = [(make_ln, qt) for qt in range(T_TILES)]
+            side_work = [(make_ln, 0), (make_m_plain, 0)] + [(make_ln, qt) for qt in range(1, T_TILES)]
             columns = 0
             for pair in range(PAIRS):
                 t, head = pair // HEADS, pair % HEADS
@@ -254,6 +259,7 @@ def tile_mhattention_own_kernel(tc, q, k, v, attn_mask, out):
             nc.vector.tensor_reduce(out=minus_g[:], in_=spread_t[:], axis=AX.X, op=ALU.max)
             regroup_v(2, turned[0])
             regroup_v(3, turned[1])
+            make_m_plain(1)
 
         work = ctx.enter_context(tc.tile_pool(name="work", bufs=3))
         u_banks = ctx.enter_context(tc.psum_pool(name="u_banks", bufs=2))
@@ -416,9 +422,9 @@ def tile_mhattention_own_kernel(tc, q, k, v, attn_mask, out):
                 work_on(j, *args)
 
         blend(0)
+        row_max_n(0)
         for half in range(HALVES):
             finish_add(0, slice(half * BANK, (half + 1) * BANK))
-        row_max_n(0)
         assemble(0)
         exponential_n(0)
         for j in range(PAIRS + 3):
@@ -447,6 +453,10 @@ def tile_mhattention_own_kernel(tc, q, k, v, attn_mask, out):
                 finish_add(j // HEADS + 1)
             if j < 3:
                 quantise_v(j + 1)
+            if j in (2, 6):
+                weigh_scores(nc.vector, VECTOR_PRODUCTS[j // 4])
+            if j in (1, 5):
+                make_m_plain(2 + j // 4)
             stage(j - 1, quantise, T)
             stage(j, reciprocal, T)
             if j == PAIRS - 1:

@@ -21,6 +21,7 @@ BANK = 512
 HALVES = SEQ // BANK
 PACK = 4
 PASSES = SEQ // (P * PACK)
+SUM_GAP = 8
 WORDS = PASSES * P
 SCALE = P ** -0.5
 FLOPS = 2 * 2 * HEADS * SEQ * SEQ * P
@@ -81,19 +82,18 @@ def tile_mhattention_own_kernel(tc, q, k, v, attn_mask, out):
                 out=m_n[:, qt, :], in_=mask_sb[T_TILES + qt][:], func=ACT.Copy, scale=1.0e-4, bias=1.0
             )
 
-        def quantise_v(head):
-            words = slice(head * WORDS, (head + 1) * WORDS)
+        def quantise_v(two):
+            words = slice(two * 2 * WORDS, (two + 1) * 2 * WORDS)
             nc.vector.quantize_mx(
-                out=v_codes[:, words].bitcast(FP8X4),
-                scales=v_scales[:, words],
-                in_=v_grouped[head][:],
+                out=v_codes[:, words].bitcast(FP8X4), scales=v_scales[:, words],
+                in_=v_grouped[two][:].rearrange("p h k -> p (h k)"),
             )
 
         stats = ctx.enter_context(tc.tile_pool(name="stats", bufs=4))
         v_grouped = {}
         mask_sb = {}
         mask_pool = ctx.enter_context(tc.tile_pool(name="masks", bufs=Q_TILES))
-        v_pool = ctx.enter_context(tc.tile_pool(name="v_pool", bufs=HEADS))
+        v_pool = ctx.enter_context(tc.tile_pool(name="v_pool", bufs=2))
 
         with ExitStack() as part1:
             loaded = part1.enter_context(tc.tile_pool(name="loaded", bufs=1))
@@ -175,12 +175,16 @@ def tile_mhattention_own_kernel(tc, q, k, v, attn_mask, out):
             pending = None
             for pair in range(PAIRS):
                 head, pr = pair // (CHUNKS // 2), pair % (CHUNKS // 2)
-                fused = pr == 3 or (pr == 1 and head < 2)
+                if pr == 3 or (pr == 1 and head < 2):
+                    by_vector = (2 * pr, 2 * pr + 1)
+                else:
+                    by_vector = (0,) if pair == 0 else ()
+                by_scalar = slice(2 * pr + len(by_vector), 2 * pr + 2)
                 for c in (2 * pr, 2 * pr + 1):
                     bank = score_bank(k_sb[:, head, c * P : (c + 1) * P], q_sb[:, head, 0:BANK])
                     place = s_t[:, head, :, c, :]
                     bank_view = bank[:].rearrange("p (t i) -> p t i", t=T_TILES)
-                    if fused:
+                    if c in by_vector:
                         nc.vector.tensor_scalar(
                             out=place, in0=bank_view, scalar1=SCALE, scalar2=None,
                             op0=ALU.mult, op1=ALU.min, accum_out=t_min[:, columns : columns + 1],
@@ -192,8 +196,8 @@ def tile_mhattention_own_kernel(tc, q, k, v, attn_mask, out):
                     settle(t_min, columns, ALU.min)
                     columns += 1
                     pending = None
-                if not fused:
-                    pending = s_t[:, head, :, 2 * pr : 2 * pr + 2, :].rearrange("p t c i -> p t (c i)")
+                if len(by_vector) < 2:
+                    pending = s_t[:, head, :, by_scalar, :].rearrange("p t c i -> p t (c i)")
                     if side_work:
                         work_on, qt = side_work.pop(0)
                         work_on(qt)
@@ -239,9 +243,12 @@ def tile_mhattention_own_kernel(tc, q, k, v, attn_mask, out):
             nc.vector.tensor_reduce(out=earlier_max[:], in_=n_max[:, 0:columns], axis=AX.X, op=ALU.max)
 
             def regroup_v(head, bank):
-                v_grouped[head] = v_pool.tile([P, PASSES * P * PACK], BF16, name="v_grouped", align_bytes=64)
+                if head % 2 == 0:
+                    v_grouped[head // 2] = v_pool.tile([P, 2, SEQ], BF16, name="v_grouped", align_bytes=64)
                 nc.scalar.copy(
-                    out=v_grouped[head][:].bitcast(F32).rearrange("p (ps d u) -> p ps d u", ps=PASSES, u=PACK // 2),
+                    out=v_grouped[head // 2][:, head % 2, :].bitcast(F32).rearrange(
+                        "p (ps d u) -> p ps d u", ps=PASSES, u=PACK // 2
+                    ),
                     in_=bank[:].rearrange("p (ps u d) -> p ps d u", ps=PASSES, u=PACK // 2),
                 )
 
@@ -261,12 +268,13 @@ def tile_mhattention_own_kernel(tc, q, k, v, attn_mask, out):
             regroup_v(3, turned[1])
             make_m_plain(1)
 
-        work = ctx.enter_context(tc.tile_pool(name="work", bufs=3))
+        work = ctx.enter_context(tc.tile_pool(name="work", bufs=2))
+        results = ctx.enter_context(tc.tile_pool(name="results", bufs=4))
         u_banks = ctx.enter_context(tc.psum_pool(name="u_banks", bufs=2))
         attn_banks = ctx.enter_context(tc.psum_pool(name="attn_banks", bufs=2))
         out_banks = ctx.enter_context(tc.psum_pool(name="out_banks", bufs=1))
         live = {}
-        T, N = "t", "n"
+        KINDS = T, N = "t", "n"
 
         def finish_add(qt, cols=slice(0, SEQ)):
             nc.vector.scalar_tensor_tensor(
@@ -314,8 +322,10 @@ def tile_mhattention_own_kernel(tc, q, k, v, attn_mask, out):
                 )
 
         def total_t(j):
-            live["sum", T, j] = stats.tile([P, 1], F32, name="sum_t")
-            nc.vector.tensor_reduce(out=live["sum", T, j][:], in_=live["sums", j][:], axis=AX.X, op=ALU.add)
+            live["pair_sums", j] = stats.tile([P, 2 * SUM_GAP], F32, name="pair_sums")
+            nc.gpsimd.tensor_tensor(
+                out=live["pair_sums", j][:, 0:1], in0=live["sums", j][:, 0:1], in1=live["sums", j][:, 1:2], op=ALU.add
+            )
 
         def blend(j):
             nc.vector.scalar_tensor_tensor(
@@ -333,39 +343,50 @@ def tile_mhattention_own_kernel(tc, q, k, v, attn_mask, out):
             )
 
         def weigh_n(j):
-            live["sum", N, j] = stats.tile([P, 1], F32, name="sum_n")
             nc.vector.scalar_tensor_tensor(
                 out=block_n(j), in0=block_n(j), scalar=1.0, in1=m_n[:, j // HEADS, :],
-                op0=ALU.mult, op1=ALU.mult, accum_out=live["sum", N, j][:],
+                op0=ALU.mult, op1=ALU.mult, accum_out=live["pair_sums", j][:, SUM_GAP : SUM_GAP + 1],
             )
 
-        def reciprocal(j, kind):
-            live["inv", kind, j] = stats.tile([P, 1], F32, name="inv_" + kind)
-            nc.vector.reciprocal(out=live["inv", kind, j][:], in_=live["sum", kind, j][:])
+        def reciprocal(j):
+            live["inv", j] = stats.tile([P, 2], F32, name="inv")
+            nc.vector.reciprocal(out=live["inv", j][:], in_=live["pair_sums", j][:, 0 : SUM_GAP + 1 : SUM_GAP])
 
-        def normalise_t(j):
-            live["attn", T, j] = work.tile([P, SEQ], BF16, name="attn_t")
+        def normalise_gpsimd(j, kind, cols):
             nc.gpsimd.tensor_scalar(
-                out=live["attn", T, j][:, 0:BANK], in0=block_t(j)[:, 0:BANK], scalar1=live["inv", T, j][:, 0:1],
-                scalar2=0.0, op0=ALU.mult, op1=ALU.add,
-            )
-            nc.scalar.activation(
-                out=live["attn", T, j][:, BANK:SEQ], in_=block_t(j)[:, BANK:SEQ], func=ACT.Copy,
-                scale=live["inv", T, j][:, 0:1],
+                out=live["attn", kind, j][:, cols], in0=rows(j, kind)[:, cols], scalar1=inverse(j, kind), scalar2=0.0,
+                op0=ALU.mult, op1=ALU.add,
             )
 
-        def normalise(j, kind, engine):
-            live["attn", kind, j] = work.tile([P, SEQ], BF16, name="attn_" + kind)
-            rows = block_t(j) if kind == T else block_n(j)
-            if engine == "scalar":
-                nc.scalar.activation(
-                    out=live["attn", kind, j][:], in_=rows, func=ACT.Copy, scale=live["inv", kind, j][:, 0:1]
-                )
+        def normalise_scalar(j, kind, cols):
+            nc.scalar.activation(
+                out=live["attn", kind, j][:, cols], in_=rows(j, kind)[:, cols], func=ACT.Copy, scale=inverse(j, kind)
+            )
+
+        def normalise_vector(j, kind, cols):
+            nc.vector.tensor_scalar(
+                out=live["attn", kind, j][:, cols], in0=rows(j, kind)[:, cols], scalar1=inverse(j, kind), scalar2=None,
+                op0=ALU.mult,
+            )
+
+        def rows(j, kind):
+            return block_t(j) if kind == T else block_n(j)
+
+        def inverse(j, kind):
+            column = 0 if kind == T else 1
+            return live["inv", j][:, column : column + 1]
+
+        def normalise(j):
+            for kind in (T, N):
+                live["attn", kind, j] = work.tile([P, SEQ], BF16, name="attn_" + kind)
+            if j < PAIRS - 1:
+                normalise_gpsimd(j, T, slice(0, BANK))
+                normalise_scalar(j, T, slice(BANK, SEQ))
+                normalise_scalar(j, N, slice(0, SEQ))
             else:
-                nc.vector.tensor_scalar(
-                    out=live["attn", kind, j][:], in0=rows, scalar1=live["inv", kind, j][:, 0:1], scalar2=None,
-                    op0=ALU.mult,
-                )
+                normalise_vector(j, T, slice(0, SEQ))
+                normalise_scalar(j, N, slice(0, BANK))
+                normalise_vector(j, N, slice(BANK, SEQ))
 
         def transpose(j, kind):
             live["attn_t", kind, j] = attn_banks.tile([P, BANK], F32, name="attn_t")
@@ -377,44 +398,58 @@ def tile_mhattention_own_kernel(tc, q, k, v, attn_mask, out):
                 )
 
         def regroup(j, kind, copy):
-            live["grouped", kind, j] = work.tile([P, SEQ], BF16, name="grouped", align_bytes=64)
+            if kind == T:
+                live["grouped", j] = work.tile([P, 2, SEQ], BF16, name="grouped", align_bytes=64)
             copy(
-                out=live["grouped", kind, j][:].bitcast(F32).rearrange("p (ps i u) -> p ps i u", ps=PASSES, u=PACK // 2),
+                out=live["grouped", j][:, KINDS.index(kind), :].bitcast(F32).rearrange(
+                    "p (ps i u) -> p ps i u", ps=PASSES, u=PACK // 2
+                ),
                 in_=live["attn_t", kind, j][:].rearrange("p (ps u i) -> p ps i u", ps=PASSES, u=PACK // 2),
             )
 
-        def quantise(j, kind):
-            live["codes", kind, j] = work.tile([P, WORDS], U32, name="codes", align_bytes=64)
-            live["scales", kind, j] = work.tile([P, WORDS], U8, name="scales", align_bytes=64)
-            nc.vector.quantize_mx(
-                out=live["codes", kind, j][:].bitcast(FP8X4), scales=live["scales", kind, j][:],
-                in_=live["grouped", kind, j][:],
-            )
-
-        def multiply(j, kind):
-            head, qt = j % HEADS, j // HEADS
-            if head == 0:
-                live["out", kind, qt] = out_banks.tile([P, HEADS * P], F32, name="out_" + kind)
-            for ps in range(PASSES):
-                v_words = slice(head * WORDS + ps * P, head * WORDS + (ps + 1) * P)
-                attn_words = slice(ps * P, (ps + 1) * P)
-                nc.tensor.matmul_mx(
-                    out=live["out", kind, qt][:, head * P : (head + 1) * P],
-                    lhsT=v_codes[:, v_words].bitcast(FP8X4), lhsT_scale=v_scales[:, v_words],
-                    rhs=live["codes", kind, j][:, attn_words].bitcast(FP8X4),
-                    rhs_scale=live["scales", kind, j][:, attn_words],
-                    start=(ps == 0), stop=(ps == PASSES - 1),
+        def quantise(j):
+            live["codes", j] = work.tile([P, 2 * WORDS], U32, name="codes", align_bytes=64)
+            live["scales", j] = work.tile([P, 2 * WORDS], U8, name="scales", align_bytes=64)
+            spans = [(0, 2)] if j < PAIRS - 1 else [(0, 1), (1, 2)]
+            for first, end in spans:
+                words = slice(first * WORDS, end * WORDS)
+                nc.vector.quantize_mx(
+                    out=live["codes", j][:, words].bitcast(FP8X4), scales=live["scales", j][:, words],
+                    in_=live["grouped", j][:, first:end, :].rearrange("p r k -> p (r k)"),
                 )
 
-        def store(j, kind):
-            if j % HEADS == HEADS - 1:
-                qt = j // HEADS
+        def multiply(j):
+            head, qt = j % HEADS, j // HEADS
+            for kind in (T, N):
+                if head == 0:
+                    live["out", kind, qt] = out_banks.tile([P, HEADS * P], F32, name="out_" + kind)
+                for ps in range(PASSES):
+                    v_words = slice(head * WORDS + ps * P, head * WORDS + (ps + 1) * P)
+                    first = KINDS.index(kind) * WORDS + ps * P
+                    nc.tensor.matmul_mx(
+                        out=live["out", kind, qt][:, head * P : (head + 1) * P],
+                        lhsT=v_codes[:, v_words].bitcast(FP8X4), lhsT_scale=v_scales[:, v_words],
+                        rhs=live["codes", j][:, first : first + P].bitcast(FP8X4),
+                        rhs_scale=live["scales", j][:, first : first + P],
+                        start=(ps == 0), stop=(ps == PASSES - 1),
+                    )
+
+        def store(j):
+            head, qt = j % HEADS, j // HEADS
+            if qt == T_TILES - 1 and head == HEADS - 2:
+                heads = slice(0, HEADS - 1)
+            elif head == HEADS - 1:
+                heads = slice(HEADS - 1 if qt == T_TILES - 1 else 0, HEADS)
+            else:
+                return
+            for kind in (T, N):
                 place = qt if kind == T else T_TILES + qt
-                out_sb = work.tile([P, HEADS * P], F32, name="out_sb")
-                nc.scalar.copy(out=out_sb[:], in_=live["out", kind, qt][:])
+                cols = slice(heads.start * P, heads.stop * P)
+                out_sb = results.tile([P, HEADS * P], F32, name="out_sb")
+                nc.scalar.copy(out=out_sb[:, cols], in_=live["out", kind, qt][:, cols])
                 nc.sync.dma_start(
-                    out=out_dram[:, :, place * P : (place + 1) * P],
-                    in_=out_sb[:].rearrange("p (n i) -> p n i", n=HEADS),
+                    out=out_dram[:, heads, place * P : (place + 1) * P],
+                    in_=out_sb[:, cols].rearrange("p (n i) -> p n i", i=P),
                 )
 
         def stage(j, work_on, *args):
@@ -425,41 +460,37 @@ def tile_mhattention_own_kernel(tc, q, k, v, attn_mask, out):
         row_max_n(0)
         for half in range(HALVES):
             finish_add(0, slice(half * BANK, (half + 1) * BANK))
+        blend(1)
+        quantise_v(1)
         assemble(0)
         exponential_n(0)
-        for j in range(PAIRS + 3):
-            copy = nc.scalar.copy if j < PAIRS else nc.vector.tensor_copy
-            if j < PAIRS:
-                stage(j - 1, normalise_t)
-            stage(j + 1, assemble)
+        row_max_t(0)
+        bias_t(0)
+        assemble(1)
+        exponential_t(0)
+        total_t(0)
+        for j in range(PAIRS + 2):
+            stage(j + 2, assemble)
             stage(j - 1, transpose, T)
-            stage(j, row_max_t)
+            stage(j - 1, transpose, N)
+            stage(j + 1, row_max_t)
+            stage(j + 2, blend)
+            stage(j + 1, bias_t)
+            stage(j + 1, exponential_t)
+            stage(j - 2, quantise)
+            stage(j - 1, regroup, T, nc.scalar.copy)
+            stage(j - 1, regroup, N, nc.scalar.copy if j < PAIRS else nc.vector.tensor_copy)
+            stage(j - 2, multiply)
             stage(j, weigh_n)
-            stage(j, bias_t)
-            stage(j, exponential_t)
-            stage(j + 1, blend)
-            stage(j, reciprocal, N)
-            stage(j, normalise, N, "scalar" if j < PAIRS - 1 else "vector")
-            stage(j - 1, quantise, N)
-            stage(j - 2, multiply, T)
-            stage(j - 1, multiply, N)
-            stage(j, transpose, N)
-            stage(j + 1, row_max_n)
-            stage(j, total_t)
-            stage(j - 1, regroup, T, copy)
-            stage(j + 1, exponential_n)
-            stage(j, regroup, N, copy)
             if j % HEADS == 1 and j // HEADS + 1 < T_TILES:
                 finish_add(j // HEADS + 1)
-            if j < 3:
-                quantise_v(j + 1)
             if j in (2, 6):
                 weigh_scores(nc.vector, VECTOR_PRODUCTS[j // 4])
             if j in (1, 5):
                 make_m_plain(2 + j // 4)
-            stage(j - 1, quantise, T)
-            stage(j, reciprocal, T)
-            if j == PAIRS - 1:
-                normalise(j, T, "vector")
-            stage(j - 1, store, N)
-            stage(j - 2, store, T)
+            stage(j + 1, row_max_n)
+            stage(j + 1, exponential_n)
+            stage(j, reciprocal)
+            stage(j, normalise)
+            stage(j + 1, total_t)
+            stage(j - 2, store)

@@ -77,6 +77,12 @@ def tile_mhattention_own_kernel(tc, q, k, v, attn_mask, out):
             rows = block_t(j)[:, cols]
             engine.tensor_tensor(out=rows, in0=rows, in1=m_of(j // HEADS)[:, cols], op=ALU.mult)
 
+        def make_m_plain_part(qt, cols):
+            nc.gpsimd.tensor_scalar(
+                out=m_n[:, qt, cols], in0=mask_sb[T_TILES + qt][:, cols], scalar1=1.0e-4, scalar2=1.0,
+                op0=ALU.mult, op1=ALU.add,
+            )
+
         def make_m_plain(qt):
             nc.scalar.activation(
                 out=m_n[:, qt, :], in_=mask_sb[T_TILES + qt][:], func=ACT.Copy, scale=1.0e-4, bias=1.0
@@ -376,17 +382,20 @@ def tile_mhattention_own_kernel(tc, q, k, v, attn_mask, out):
             column = 0 if kind == T else 1
             return live["inv", j][:, column : column + 1]
 
-        def normalise(j):
+        def normalise_first(j):
             for kind in (T, N):
                 live["attn", kind, j] = work.tile([P, SEQ], BF16, name="attn_" + kind)
-            if j < PAIRS - 1:
-                normalise_gpsimd(j, T, slice(0, BANK))
-                normalise_scalar(j, T, slice(BANK, SEQ))
-                normalise_scalar(j, N, slice(0, SEQ))
+            if j < PAIRS - 2:
+                own = BANK if j < 10 else SEQ
+                normalise_gpsimd(j, T, slice(0, own))
+                if own < SEQ:
+                    normalise_scalar(j, T, slice(own, SEQ))
             else:
                 normalise_vector(j, T, slice(0, SEQ))
-                normalise_scalar(j, N, slice(0, BANK))
                 normalise_vector(j, N, slice(BANK, SEQ))
+
+        def normalise_second(j):
+            normalise_scalar(j, N, slice(0, SEQ if j < PAIRS - 2 else BANK))
 
         def transpose(j, kind):
             live["attn_t", kind, j] = attn_banks.tile([P, BANK], F32, name="attn_t")
@@ -469,7 +478,30 @@ def tile_mhattention_own_kernel(tc, q, k, v, attn_mask, out):
         assemble(1)
         exponential_t(0)
         total_t(0)
+        halves = [slice(i * BANK, (i + 1) * BANK) for i in range(2)]
+        quarters = [slice(i * BANK // 2, (i + 1) * BANK // 2) for i in range(4)]
+
+        def scale_m(qt, cols):
+            nc.gpsimd.tensor_scalar(
+                out=m_of(qt)[:, cols], in0=m_of(qt)[:, cols], scalar1=minus_g[:, 0:1], scalar2=0.0,
+                op0=ALU.mult, op1=ALU.add,
+            )
+
+        def add_m(qt, cols):
+            nc.gpsimd.tensor_tensor(
+                out=add_of(qt)[:, cols], in0=add_of(qt)[:, cols], in1=m_of(qt)[:, cols], op=ALU.add
+            )
+
+        pieces = []
+        for qt in range(2, T_TILES):
+            pieces += [(weigh_scores, nc.gpsimd, VECTOR_PRODUCTS[qt - 2], cols) for cols in quarters]
+            pieces += [(scale_m, qt, cols) for cols in halves]
+            pieces += [(add_m, qt, cols) for cols in quarters]
+            pieces += [(make_m_plain_part, qt, cols) for cols in halves]
+
         for j in range(PAIRS + 2):
+            if j == PAIRS - 2:
+                row_max_n(j + 1)
             stage(j + 2, assemble)
             stage(j - 1, transpose, T)
             stage(j - 1, transpose, N)
@@ -477,20 +509,26 @@ def tile_mhattention_own_kernel(tc, q, k, v, attn_mask, out):
             stage(j + 2, blend)
             stage(j + 1, bias_t)
             stage(j + 1, exponential_t)
-            stage(j - 2, quantise)
+            if j == PAIRS - 2:
+                exponential_n(j + 1)
+            if j >= PAIRS:
+                stage(j - 2, quantise)
             stage(j - 1, regroup, T, nc.scalar.copy)
             stage(j - 1, regroup, N, nc.scalar.copy if j < PAIRS else nc.vector.tensor_copy)
-            stage(j - 2, multiply)
             stage(j, weigh_n)
-            if j % HEADS == 1 and j // HEADS + 1 < T_TILES:
-                finish_add(j // HEADS + 1)
-            if j in (2, 6):
-                weigh_scores(nc.vector, VECTOR_PRODUCTS[j // 4])
-            if j in (1, 5):
-                make_m_plain(2 + j // 4)
-            stage(j + 1, row_max_n)
-            stage(j + 1, exponential_n)
+            if j == 1:
+                finish_add(1)
+            if j < PAIRS:
+                stage(j - 2, quantise)
+            stage(j - 2, multiply)
             stage(j, reciprocal)
-            stage(j, normalise)
+            stage(j, normalise_first)
+            if j < PAIRS - 2:
+                row_max_n(j + 1)
+                exponential_n(j + 1)
+            stage(j, normalise_second)
+            for piece in pieces[0 : 3 if j in (0, 1, 6, 7) else 2]:
+                piece[0](*piece[1:])
+                pieces.remove(piece)
             stage(j + 1, total_t)
             stage(j - 2, store)

@@ -386,10 +386,8 @@ def tile_mhattention_own_kernel(tc, q, k, v, attn_mask, out):
             for kind in (T, N):
                 live["attn", kind, j] = work.tile([P, SEQ], BF16, name="attn_" + kind)
             if j < PAIRS - 2:
-                own = BANK if j < 10 else SEQ
-                normalise_gpsimd(j, T, slice(0, own))
-                if own < SEQ:
-                    normalise_scalar(j, T, slice(own, SEQ))
+                normalise_gpsimd(j, T, slice(0, BANK))
+                normalise_scalar(j, T, slice(BANK, SEQ))
             else:
                 normalise_vector(j, T, slice(0, SEQ))
                 normalise_vector(j, N, slice(BANK, SEQ))
@@ -481,23 +479,10 @@ def tile_mhattention_own_kernel(tc, q, k, v, attn_mask, out):
         halves = [slice(i * BANK, (i + 1) * BANK) for i in range(2)]
         quarters = [slice(i * BANK // 2, (i + 1) * BANK // 2) for i in range(4)]
 
-        def scale_m(qt, cols):
-            nc.gpsimd.tensor_scalar(
-                out=m_of(qt)[:, cols], in0=m_of(qt)[:, cols], scalar1=minus_g[:, 0:1], scalar2=0.0,
-                op0=ALU.mult, op1=ALU.add,
-            )
-
-        def add_m(qt, cols):
-            nc.gpsimd.tensor_tensor(
-                out=add_of(qt)[:, cols], in0=add_of(qt)[:, cols], in1=m_of(qt)[:, cols], op=ALU.add
-            )
-
         pieces = []
-        for qt in range(2, T_TILES):
-            pieces += [(weigh_scores, nc.gpsimd, VECTOR_PRODUCTS[qt - 2], cols) for cols in quarters]
-            pieces += [(scale_m, qt, cols) for cols in halves]
-            pieces += [(add_m, qt, cols) for cols in quarters]
-            pieces += [(make_m_plain_part, qt, cols) for cols in halves]
+        for j in VECTOR_PRODUCTS:
+            pieces += [(weigh_scores, nc.gpsimd, j, cols) for cols in quarters]
+            pieces += [(make_m_plain_part, t, cols) for t in range(2, T_TILES) for cols in halves if j == VECTOR_PRODUCTS[0]]
 
         for j in range(PAIRS + 2):
             if j == PAIRS - 2:
@@ -516,8 +501,8 @@ def tile_mhattention_own_kernel(tc, q, k, v, attn_mask, out):
             stage(j - 1, regroup, T, nc.scalar.copy)
             stage(j - 1, regroup, N, nc.scalar.copy if j < PAIRS else nc.vector.tensor_copy)
             stage(j, weigh_n)
-            if j == 1:
-                finish_add(1)
+            if j % HEADS == 1 and j // HEADS + 1 < T_TILES:
+                finish_add(j // HEADS + 1)
             if j < PAIRS:
                 stage(j - 2, quantise)
             stage(j - 2, multiply)
@@ -527,8 +512,8 @@ def tile_mhattention_own_kernel(tc, q, k, v, attn_mask, out):
                 row_max_n(j + 1)
                 exponential_n(j + 1)
             stage(j, normalise_second)
-            for piece in pieces[0 : 3 if j in (0, 1, 6, 7) else 2]:
+            if pieces:
+                piece = pieces.pop(0)
                 piece[0](*piece[1:])
-                pieces.remove(piece)
             stage(j + 1, total_t)
             stage(j - 2, store)

@@ -386,14 +386,17 @@ def tile_mhattention_own_kernel(tc, q, k, v, attn_mask, out):
             for kind in (T, N):
                 live["attn", kind, j] = work.tile([P, SEQ], BF16, name="attn_" + kind)
             if j < PAIRS - 2:
-                normalise_gpsimd(j, T, slice(0, BANK))
-                normalise_scalar(j, T, slice(BANK, SEQ))
+                share = BANK if pieces else SEQ
+                normalise_gpsimd(j, T, slice(0, share))
+                if share < SEQ:
+                    normalise_scalar(j, T, slice(share, SEQ))
             else:
                 normalise_vector(j, T, slice(0, SEQ))
-                normalise_vector(j, N, slice(BANK, SEQ))
+                normalise_vector(j, N, slice(BANK if j == PAIRS - 1 else 0, SEQ))
 
         def normalise_second(j):
-            normalise_scalar(j, N, slice(0, SEQ if j < PAIRS - 2 else BANK))
+            if j != PAIRS - 2:
+                normalise_scalar(j, N, slice(0, SEQ if j < PAIRS - 2 else BANK))
 
         def transpose(j, kind):
             live["attn_t", kind, j] = attn_banks.tile([P, BANK], F32, name="attn_t")
@@ -487,6 +490,7 @@ def tile_mhattention_own_kernel(tc, q, k, v, attn_mask, out):
         for j in range(PAIRS + 2):
             if j == PAIRS - 2:
                 row_max_n(j + 1)
+                exponential_n(j + 1)
             stage(j + 2, assemble)
             stage(j - 1, transpose, T)
             stage(j - 1, transpose, N)
@@ -494,8 +498,6 @@ def tile_mhattention_own_kernel(tc, q, k, v, attn_mask, out):
             stage(j + 2, blend)
             stage(j + 1, bias_t)
             stage(j + 1, exponential_t)
-            if j == PAIRS - 2:
-                exponential_n(j + 1)
             if j >= PAIRS:
                 stage(j - 2, quantise)
             stage(j - 1, regroup, T, nc.scalar.copy)

from contextlib import ExitStack

import concourse.mybir as mybir
from concourse.masks import make_identity

F32 = mybir.dt.float32
BF16 = mybir.dt.bfloat16
U32 = mybir.dt.uint32
U8 = mybir.dt.uint8
FP8X4 = mybir.dt.float8_e4m3fn_x4
ALU = mybir.AluOpType
ACT = mybir.ActivationFunctionType
AX = mybir.AxisListType

P = 128
HEADS = 4
SEQ = 1024
Q_TILES = SEQ // P
CHUNKS = SEQ // P
BANK = 512
HALVES = SEQ // BANK
PACK = 4
PASSES = SEQ // (P * PACK)
SUM_GAP = 8
WORDS = PASSES * P
SCALE = P ** -0.5
FLOPS = 2 * 2 * HEADS * SEQ * SEQ * P

T_TILES = Q_TILES // 2
VECTOR_PRODUCTS = (11, 15)
PAIRS = T_TILES * HEADS


def tile_mhattention_own_kernel(tc, q, k, v, attn_mask, out):
    nc = tc.nc
    q_dram = q.rearrange("b c h w -> (b c) (h w)").rearrange("(n d) s -> d n s", d=P)
    k_dram = k.rearrange("b c h w -> (b c) (h w)").rearrange("(n d) s -> d n s", d=P)
    v_dram = v.rearrange("b c h w -> (b c) (h w)").rearrange("(n d) s -> d n s", d=P)
    out_dram = out.rearrange("b c h w -> (b c) (h w)").rearrange("(n d) s -> d n s", d=P)
    mask_dram = attn_mask.rearrange("b i j -> (b i) j").rearrange("(qt p) j -> p qt j", p=P)

    with ExitStack() as ctx:
        ctx.enter_context(tc.manual_schedule())
        keep = ctx.enter_context(tc.tile_pool(name="keep", bufs=1))

        s_t = keep.tile([P, HEADS, T_TILES, CHUNKS, P], F32)
        s_n = keep.tile([P, T_TILES, HEADS, SEQ], F32)
        m_t = keep.tile([P, T_TILES, CHUNKS, P], F32)
        m_n = keep.tile([P, T_TILES, SEQ], F32)
        add_t = keep.tile([P, T_TILES, CHUNKS, P], F32)
        v_codes = keep.tile([P, HEADS * WORDS], U32, align_bytes=64)
        v_scales = keep.tile([P, HEADS * WORDS], U8, align_bytes=64)
        ident_bf16 = keep.tile([P, P], BF16)
        ident_f32 = keep.tile([P, P], F32)
        minus_g = keep.tile([P, 1], F32)
        one = keep.tile([P, 1], F32)
        ln_of_one = keep.tile([P, 1], F32)

        nc.vector.memset(one[:], 1.0)
        nc.scalar.activation(out=ln_of_one[:], in_=one[:], func=ACT.Ln)
        make_identity(nc, ident_bf16[:])
        make_identity(nc, ident_f32[:])

        def block_t(j):
            return s_t[:, j % HEADS, j // HEADS].rearrange("p c i -> p (c i)")

        def block_n(j):
            return s_n[:, j // HEADS, j % HEADS, :]

        def m_of(qt):
            return m_t[:, qt].rearrange("p c i -> p (c i)")

        def add_of(qt):
            return add_t[:, qt].rearrange("p c i -> p (c i)")

        def weigh_scores(engine, j, cols=slice(0, SEQ)):
            rows = block_t(j)[:, cols]
            engine.tensor_tensor(out=rows, in0=rows, in1=m_of(j // HEADS)[:, cols], op=ALU.mult)

        def make_m_plain_part(qt, cols):
            nc.gpsimd.tensor_scalar(
                out=m_n[:, qt, cols], in0=mask_sb[T_TILES + qt][:, cols], scalar1=1.0e-4, scalar2=1.0,
                op0=ALU.mult, op1=ALU.add,
            )

        def make_m_plain(qt):
            nc.scalar.activation(
                out=m_n[:, qt, :], in_=mask_sb[T_TILES + qt][:], func=ACT.Copy, scale=1.0e-4, bias=1.0
            )

        def quantise_v(two):
            words = slice(two * 2 * WORDS, (two + 1) * 2 * WORDS)
            nc.vector.quantize_mx(
                out=v_codes[:, words].bitcast(FP8X4), scales=v_scales[:, words],
                in_=v_grouped[two][:].rearrange("p h k -> p (h k)"),
            )

        stats = ctx.enter_context(tc.tile_pool(name="stats", bufs=4))
        v_grouped = {}
        mask_sb = {}
        mask_pool = ctx.enter_context(tc.tile_pool(name="masks", bufs=Q_TILES))
        v_pool = ctx.enter_context(tc.tile_pool(name="v_pool", bufs=2))

        with ExitStack() as part1:
            loaded = part1.enter_context(tc.tile_pool(name="loaded", bufs=1))
            score_banks = part1.enter_context(tc.psum_pool(name="score_banks", bufs=5))
            turned_banks = part1.enter_context(tc.psum_pool(name="turned_banks", bufs=2))
            max_bank = part1.enter_context(tc.psum_pool(name="max_bank", bufs=1))
            q_sb = loaded.tile([P, HEADS, SEQ], BF16)
            k_sb = loaded.tile([P, HEADS, SEQ], BF16)
            v_sb = loaded.tile([P, HEADS, SEQ], BF16)
            t_min = loaded.tile([P, 2 * PAIRS], F32)
            n_max = loaded.tile([P, PAIRS + PAIRS // 4], F32)
            t_top = loaded.tile([P, 1], F32)
            earlier_max = loaded.tile([P, 1], F32)
            last_max = loaded.tile([P, 1], F32)
            spread = loaded.tile([P, P], F32)

            def load_mask(qt):
                mask_sb[qt] = mask_pool.tile([P, SEQ], BF16, name="mask_sb")
                nc.sync.dma_start(out=mask_sb[qt][:], in_=mask_dram[:, qt, :])

            first_k = 2 * P
            nc.sync.dma_start(out=k_sb[:, 0, 0:first_k], in_=k_dram[:, 0, 0:first_k])
            nc.sync.dma_start(out=q_sb[:, 0, 0:BANK], in_=q_dram[:, 0, 0:BANK])
            nc.sync.dma_start(out=k_sb[:, 0, first_k:SEQ], in_=k_dram[:, 0, first_k:SEQ])
            load_mask(0)
            load_mask(1)
            for head in range(1, HEADS):
                nc.sync.dma_start(out=q_sb[:, head, 0:BANK], in_=q_dram[:, head, 0:BANK])
                nc.sync.dma_start(out=k_sb[:, head, :], in_=k_dram[:, head, :])
                if head < 3:
                    load_mask(head + 1)
            nc.sync.dma_start(out=q_sb[:, :, BANK:SEQ], in_=q_dram[:, :, BANK:SEQ])
            for qt in range(4, Q_TILES):
                load_mask(qt)
            nc.sync.dma_start(out=v_sb[:], in_=v_dram)

            def turn(source):
                bank = turned_banks.tile([P, SEQ], BF16, name="turned")
                for c in range(CHUNKS):
                    nc.tensor.transpose(
                        out=bank[:, c * P : (c + 1) * P], in_=source[:, c * P : (c + 1) * P], identity=ident_bf16[:]
                    )
                return bank

            def turn_words(source):
                bank = turned_banks.tile([P, BANK], F32, name="turned")
                for c in range(BANK // P):
                    cols = slice(c * P, (c + 1) * P)
                    nc.tensor.transpose(out=bank[:, cols], in_=source.bitcast(F32)[:, cols], identity=ident_f32[:])
                return bank

            def make_m(qt):
                bank = turn(mask_sb[qt][:])
                nc.scalar.activation(out=m_of(qt), in_=bank[:], func=ACT.Copy, scale=1.0e-4, bias=1.0)

            def make_ln(qt):
                nc.scalar.activation(out=add_of(qt), in_=m_of(qt), func=ACT.Ln)

            def score_bank(lhs, rhs):
                bank = score_banks.tile([P, BANK], F32, name="bank")
                nc.tensor.matmul(out=bank[:], lhsT=lhs, rhs=rhs, start=True, stop=True)
                return bank

            def settle(stat, column, op):
                nc.vector.tensor_reduce(out=stat[:, column : column + 1], in_=pending, axis=AX.XY, op=op)

            side_work = [(make_m, qt) for qt in range(T_TILES)]
            to_weigh = []
            for head in range(HEADS):
                pairs_of_head = [1, 3] if head == 0 else [3]
                for i, pr in enumerate(pairs_of_head):
                    width = SEQ // len(pairs_of_head)
                    for t in range(T_TILES):
                        j = t * HEADS + head
                        if j not in VECTOR_PRODUCTS:
                            to_weigh.append((head * (CHUNKS // 2) + pr, t, j, slice(i * width, (i + 1) * width)))
            made_m = []
            columns = 0
            pending = None
            for pair in range(PAIRS):
                head, pr = pair // (CHUNKS // 2), pair % (CHUNKS // 2)
                if pr == 3 or (pr == 1 and head < 2):
                    by_vector = (2 * pr, 2 * pr + 1)
                else:
                    by_vector = (0,) if pair == 0 else ()
                by_scalar = slice(2 * pr + len(by_vector), 2 * pr + 2)
                for c in (2 * pr, 2 * pr + 1):
                    bank = score_bank(k_sb[:, head, c * P : (c + 1) * P], q_sb[:, head, 0:BANK])
                    place = s_t[:, head, :, c, :]
                    bank_view = bank[:].rearrange("p (t i) -> p t i", t=T_TILES)
                    if c in by_vector:
                        nc.vector.tensor_scalar(
                            out=place, in0=bank_view, scalar1=SCALE, scalar2=None,
                            op0=ALU.mult, op1=ALU.min, accum_out=t_min[:, columns : columns + 1],
                        )
                        columns += 1
                    else:
                        nc.scalar.activation(out=place, in_=bank_view, func=ACT.Copy, scale=SCALE)
                if pending is not None:
                    settle(t_min, columns, ALU.min)
                    columns += 1
                    pending = None
                if len(by_vector) < 2:
                    pending = s_t[:, head, :, by_scalar, :].rearrange("p t c i -> p t (c i)")
                    if side_work:
                        work_on, qt = side_work.pop(0)
                        work_on(qt)
                        made_m.append(qt)
                while to_weigh and to_weigh[0][0] <= pair and to_weigh[0][1] in made_m:
                    after, t, j, cols = to_weigh.pop(0)
                    weigh_scores(nc.gpsimd, j, cols)
            nc.vector.tensor_reduce(out=t_top[:], in_=t_min[:, 0:columns], axis=AX.X, op=ALU.min)
            side_work = [(make_ln, 0), (make_m_plain, 0)] + [(make_ln, qt) for qt in range(1, T_TILES)]
            columns = 0
            for pair in range(PAIRS):
                t, head = pair // HEADS, pair % HEADS
                fused = pair % 4 == 3
                queries = slice((T_TILES + t) * P, (T_TILES + t + 1) * P)
                for half in range(HALVES):
                    keys = slice(half * BANK, (half + 1) * BANK)
                    bank = score_bank(q_sb[:, head, queries], k_sb[:, head, keys])
                    place = s_n[:, t, head, keys]
                    if fused:
                        last = pair == PAIRS - 1 and half == HALVES - 1
                        if last:
                            settle(n_max, columns, ALU.max)
                            columns += 1
                            pending = None
                        nc.vector.tensor_scalar(
                            out=place, in0=bank[:], scalar1=-SCALE, scalar2=None, op0=ALU.mult, op1=ALU.max,
                            accum_out=last_max[:] if last else n_max[:, columns : columns + 1],
                        )
                        columns += 0 if last else 1
                    else:
                        nc.scalar.activation(out=place, in_=bank[:], func=ACT.Copy, scale=-SCALE)
                if pending is not None:
                    settle(n_max, columns, ALU.max)
                    columns += 1
                    pending = None
                if not fused:
                    pending = s_n[:, t, head, :].rearrange("p (c i) -> p c i", i=P)
                    if side_work and pair >= 4:
                        work_on, qt = side_work.pop(0)
                        work_on(qt)
                if pair == 0:
                    nc.vector.tensor_scalar(out=t_top[:], in0=t_top[:], scalar1=-1.0, scalar2=None, op0=ALU.mult)
            nc.vector.tensor_reduce(out=earlier_max[:], in_=n_max[:, 0:columns], axis=AX.X, op=ALU.max)

            def regroup_v(head, bank):
                if head % 2 == 0:
                    v_grouped[head // 2] = v_pool.tile([P, 2, SEQ], BF16, name="v_grouped", align_bytes=64)
                nc.scalar.copy(
                    out=v_grouped[head // 2][:, head % 2, :].bitcast(F32).rearrange(
                        "p (ps d u) -> p ps d u", ps=PASSES, u=PACK // 2
                    ),
                    in_=bank[:].rearrange("p (ps u d) -> p ps d u", ps=PASSES, u=PACK // 2),
                )

            turned = [turn_words(v_sb[:, head, :]) for head in range(2)]
            regroup_v(0, turned[0])
            regroup_v(1, turned[1])
            turned = [turn_words(v_sb[:, head, :]) for head in range(2, 4)]
            nc.vector.tensor_scalar(
                out=spread[:], in0=last_max[:, 0:1].to_broadcast([P, P]),
                scalar1=earlier_max[:, 0:1], scalar2=t_top[:, 0:1], op0=ALU.max, op1=ALU.max,
            )
            spread_t = max_bank.tile([P, P], F32)
            nc.tensor.transpose(out=spread_t[:], in_=spread[:], identity=ident_f32[:])
            quantise_v(0)
            nc.vector.tensor_reduce(out=minus_g[:], in_=spread_t[:], axis=AX.X, op=ALU.max)
            regroup_v(2, turned[0])
            regroup_v(3, turned[1])
            make_m_plain(1)

        work = ctx.enter_context(tc.tile_pool(name="work", bufs=2))
        results = ctx.enter_context(tc.tile_pool(name="results", bufs=4))
        u_banks = ctx.enter_context(tc.psum_pool(name="u_banks", bufs=2))
        attn_banks = ctx.enter_context(tc.psum_pool(name="attn_banks", bufs=2))
        out_banks = ctx.enter_context(tc.psum_pool(name="out_banks", bufs=1))
        live = {}
        KINDS = T, N = "t", "n"

        def finish_add(qt, cols=slice(0, SEQ)):
            nc.vector.scalar_tensor_tensor(
                out=add_of(qt)[:, cols], in0=m_of(qt)[:, cols], scalar=minus_g[:, 0:1], in1=add_of(qt)[:, cols],
                op0=ALU.mult, op1=ALU.add,
            )

        def assemble(j):
            qt, head = j // HEADS, j % HEADS
            for half in range(HALVES):
                bank = u_banks.tile([P, BANK], F32, name="u%d" % half)
                live["u", j, half] = bank
                for c in range(BANK // P):
                    cols = slice(c * P, (c + 1) * P)
                    chunk = half * (BANK // P) + c
                    nc.tensor.matmul(
                        out=bank[:, cols], lhsT=s_t[:, head, qt, chunk, :], rhs=ident_f32[:],
                        is_transpose=True, start=True, stop=False,
                    )
                    nc.tensor.matmul(
                        out=bank[:, cols], lhsT=add_t[:, qt, chunk, :], rhs=ident_f32[:],
                        is_transpose=True, start=False, stop=True,
                    )

        def row_max_t(j):
            live["top", j] = stats.tile([P, HALVES], F32, name="top")
            for half in range(HALVES):
                nc.vector.tensor_reduce(
                    out=live["top", j][:, half : half + 1], in_=live["u", j, half][:], axis=AX.X, op=ALU.max
                )

        def bias_t(j):
            live["bias", T, j] = stats.tile([P, 1], F32, name="bias_t")
            nc.vector.tensor_scalar(
                out=live["bias", T, j][:], in0=live["top", j][:, 0:1], scalar1=live["top", j][:, 1:2], scalar2=-1.0,
                op0=ALU.max, op1=ALU.mult,
            )

        def exponential_t(j):
            live["sums", j] = stats.tile([P, HALVES], F32, name="sums")
            for half in range(HALVES):
                nc.scalar.activation(
                    out=block_t(j)[:, half * BANK : (half + 1) * BANK], in_=live["u", j, half][:], func=ACT.Exp,
                    bias=live["bias", T, j][:, 0:1], scale=1.0, accum_out=live["sums", j][:, half : half + 1],
                )

        def total_t(j):
            live["pair_sums", j] = stats.tile([P, 2 * SUM_GAP], F32, name="pair_sums")
            nc.gpsimd.tensor_tensor(
                out=live["pair_sums", j][:, 0:1], in0=live["sums", j][:, 0:1], in1=live["sums", j][:, 1:2], op=ALU.add
            )

        def blend(j):
            nc.vector.scalar_tensor_tensor(
                out=block_n(j), in0=block_n(j), scalar=minus_g[:, 0:1], in1=m_n[:, j // HEADS, :],
                op0=ALU.subtract, op1=ALU.mult,
            )

        def row_max_n(j):
            live["bias", N, j] = stats.tile([P, 1], F32, name="bias_n")
            nc.vector.tensor_reduce(out=live["bias", N, j][:], in_=block_n(j), axis=AX.X, op=ALU.min)

        def exponential_n(j):
            nc.scalar.activation(
                out=block_n(j), in_=block_n(j), func=ACT.Exp, bias=live["bias", N, j][:, 0:1], scale=-1.0
            )

        def weigh_n(j):
            nc.vector.scalar_tensor_tensor(
                out=block_n(j), in0=block_n(j), scalar=1.0, in1=m_n[:, j // HEADS, :],
                op0=ALU.mult, op1=ALU.mult, accum_out=live["pair_sums", j][:, SUM_GAP : SUM_GAP + 1],
            )

        def reciprocal(j):
            live["inv", j] = stats.tile([P, 2], F32, name="inv")
            nc.vector.reciprocal(out=live["inv", j][:], in_=live["pair_sums", j][:, 0 : SUM_GAP + 1 : SUM_GAP])

        def normalise_gpsimd(j, kind, cols):
            nc.gpsimd.tensor_scalar(
                out=live["attn", kind, j][:, cols], in0=rows(j, kind)[:, cols], scalar1=inverse(j, kind), scalar2=0.0,
                op0=ALU.mult, op1=ALU.add,
            )

        def normalise_scalar(j, kind, cols):
            nc.scalar.activation(
                out=live["attn", kind, j][:, cols], in_=rows(j, kind)[:, cols], func=ACT.Copy, scale=inverse(j, kind)
            )

        def normalise_vector(j, kind, cols):
            nc.vector.tensor_scalar(
                out=live["attn", kind, j][:, cols], in0=rows(j, kind)[:, cols], scalar1=inverse(j, kind), scalar2=None,
                op0=ALU.mult,
            )

        def rows(j, kind):
            return block_t(j) if kind == T else block_n(j)

        def inverse(j, kind):
            column = 0 if kind == T else 1
            return live["inv", j][:, column : column + 1]

        def normalise_first(j):
            for kind in (T, N):
                live["attn", kind, j] = work.tile([P, SEQ], BF16, name="attn_" + kind)
            if j < PAIRS - 2:
                share = BANK if pieces else SEQ
                normalise_gpsimd(j, T, slice(0, share))
                if share < SEQ:
                    normalise_scalar(j, T, slice(share, SEQ))
            else:
                normalise_vector(j, T, slice(0, SEQ))
                normalise_vector(j, N, slice(BANK if j == PAIRS - 1 else 0, SEQ))

        def normalise_second(j):
            if j != PAIRS - 2:
                normalise_scalar(j, N, slice(0, SEQ if j < PAIRS - 2 else BANK))

        def transpose(j, kind):
            live["attn_t", kind, j] = attn_banks.tile([P, BANK], F32, name="attn_t")
            for c in range(BANK // P):
                cols = slice(c * P, (c + 1) * P)
                nc.tensor.transpose(
                    out=live["attn_t", kind, j][:, cols], in_=live["attn", kind, j][:].bitcast(F32)[:, cols],
                    identity=ident_f32[:],
                )

        def regroup(j, kind, copy):
            if kind == T:
                live["grouped", j] = work.tile([P, 2, SEQ], BF16, name="grouped", align_bytes=64)
            copy(
                out=live["grouped", j][:, KINDS.index(kind), :].bitcast(F32).rearrange(
                    "p (ps i u) -> p ps i u", ps=PASSES, u=PACK // 2
                ),
                in_=live["attn_t", kind, j][:].rearrange("p (ps u i) -> p ps i u", ps=PASSES, u=PACK // 2),
            )

        def quantise(j):
            live["codes", j] = work.tile([P, 2 * WORDS], U32, name="codes", align_bytes=64)
            live["scales", j] = work.tile([P, 2 * WORDS], U8, name="scales", align_bytes=64)
            spans = [(0, 2)] if j < PAIRS - 1 else [(0, 1), (1, 2)]
            for first, end in spans:
                words = slice(first * WORDS, end * WORDS)
                nc.vector.quantize_mx(
                    out=live["codes", j][:, words].bitcast(FP8X4), scales=live["scales", j][:, words],
                    in_=live["grouped", j][:, first:end, :].rearrange("p r k -> p (r k)"),
                )

        def multiply(j):
            head, qt = j % HEADS, j // HEADS
            for kind in (T, N):
                if head == 0:
                    live["out", kind, qt] = out_banks.tile([P, HEADS * P], F32, name="out_" + kind)
                for ps in range(PASSES):
                    v_words = slice(head * WORDS + ps * P, head * WORDS + (ps + 1) * P)
                    first = KINDS.index(kind) * WORDS + ps * P
                    nc.tensor.matmul_mx(
                        out=live["out", kind, qt][:, head * P : (head + 1) * P],
                        lhsT=v_codes[:, v_words].bitcast(FP8X4), lhsT_scale=v_scales[:, v_words],
                        rhs=live["codes", j][:, first : first + P].bitcast(FP8X4),
                        rhs_scale=live["scales", j][:, first : first + P],
                        start=(ps == 0), stop=(ps == PASSES - 1),
                    )

        def store(j):
            head, qt = j % HEADS, j // HEADS
            if qt == T_TILES - 1 and head == HEADS - 2:
                heads = slice(0, HEADS - 1)
            elif head == HEADS - 1:
                heads = slice(HEADS - 1 if qt == T_TILES - 1 else 0, HEADS)
            else:
                return
            for kind in (T, N):
                place = qt if kind == T else T_TILES + qt
                cols = slice(heads.start * P, heads.stop * P)
                out_sb = results.tile([P, HEADS * P], F32, name="out_sb")
                nc.scalar.copy(out=out_sb[:, cols], in_=live["out", kind, qt][:, cols])
                nc.sync.dma_start(
                    out=out_dram[:, heads, place * P : (place + 1) * P],
                    in_=out_sb[:, cols].rearrange("p (n i) -> p n i", i=P),
                )

        def stage(j, work_on, *args):
            if 0 <= j < PAIRS:
                work_on(j, *args)

        blend(0)
        row_max_n(0)
        for half in range(HALVES):
            finish_add(0, slice(half * BANK, (half + 1) * BANK))
        blend(1)
        quantise_v(1)
        assemble(0)
        exponential_n(0)
        row_max_t(0)
        bias_t(0)
        assemble(1)
        exponential_t(0)
        total_t(0)
        halves = [slice(i * BANK, (i + 1) * BANK) for i in range(2)]
        quarters = [slice(i * BANK // 2, (i + 1) * BANK // 2) for i in range(4)]

        pieces = []
        for j in VECTOR_PRODUCTS:
            pieces += [(weigh_scores, nc.gpsimd, j, cols) for cols in quarters]
            pieces += [(make_m_plain_part, t, cols) for t in range(2, T_TILES) for cols in halves if j == VECTOR_PRODUCTS[0]]

        for j in range(PAIRS + 2):
            if j == PAIRS - 2:
                row_max_n(j + 1)
                exponential_n(j + 1)
            stage(j + 2, assemble)
            stage(j - 1, transpose, T)
            stage(j - 1, transpose, N)
            stage(j + 1, row_max_t)
            stage(j + 2, blend)
            stage(j + 1, bias_t)
            stage(j + 1, exponential_t)
            if j >= PAIRS:
                stage(j - 2, quantise)
            stage(j - 1, regroup, T, nc.scalar.copy)
            stage(j - 1, regroup, N, nc.scalar.copy if j < PAIRS else nc.vector.tensor_copy)
            stage(j, weigh_n)
            if j % HEADS == 1 and j // HEADS + 1 < T_TILES:
                finish_add(j // HEADS + 1)
            if j < PAIRS:
                stage(j - 2, quantise)
            stage(j - 2, multiply)
            stage(j, reciprocal)
            stage(j, normalise_first)
            if j < PAIRS - 2:
                row_max_n(j + 1)
                exponential_n(j + 1)
            stage(j, normalise_second)
            if pieces:
                piece = pieces.pop(0)
                piece[0](*piece[1:])
            stage(j + 1, total_t)
            stage(j - 2, store)
